import numpy as np
import ml_dtypes


def mxq(x, axis, fmt="e4m3"):
    dtype, down = {"e4m3": (ml_dtypes.float8_e4m3fn, 7), "e5m2": (ml_dtypes.float8_e5m2, 14)}[fmt]
    v = np.moveaxis(np.asarray(x, np.float32).astype(ml_dtypes.bfloat16).astype(np.float64), axis, -1)
    blocks = v.reshape(v.shape[:-1] + (-1, 32))
    amax = np.abs(blocks).max(-1, keepdims=True)
    byte = np.maximum(np.where(amax > 0, np.frexp(amax)[1] - 1 + 127, 0) - down, 1)
    scale = np.exp2(byte - 127.0)
    codes = (blocks / scale).astype(np.float32).astype(dtype).astype(np.float64)
    return np.moveaxis((codes * scale).reshape(v.shape), -1, axis)


WIDE = False


def mx_kscale(k):
    if not WIDE:
        return np.ones(k)
    levels = np.array([18, -18])
    if k % 512:
        return np.exp2(np.random.permutation(np.resize(levels, k // 32))).repeat(32)
    a = np.empty((k // 512, 16))
    for p in range(k // 512):
        a[p, :8] = np.random.permutation(np.resize(levels, 8))
        for g in range(8):
            far = levels[np.abs(levels - a[p, g]) >= 10]
            a[p, g + 8] = far[np.random.randint(len(far))]
    return np.exp2(a.ravel()).repeat(32)


BF16 = ml_dtypes.bfloat16


def bf(x):
    return np.asarray(x, np.float32).astype(BF16)


def f64(x):
    return np.asarray(x).astype(np.float64)


B, E, D1, D2, WS1, WS2, H = 2, 1024, 32, 16, 8, 8, 32
NW = (D1 // WS1) * (D2 // WS2)
S = WS1 * WS2
DH = E // H
T = B * NW * S


def to_image(v):
    c = v.shape[-1]
    v = v.reshape(B, D1 // WS1, D2 // WS2, WS1, WS2, c).transpose(0, 1, 3, 2, 4, 5).reshape(B, D1, D2, c)
    return np.roll(v, (WS1 // 2, WS2 // 2), axis=(1, 2))


def to_windows(g):
    c = g.shape[-1]
    g = np.roll(g, (-(WS1 // 2), -(WS2 // 2)), axis=(1, 2))
    return g.reshape(B, D1 // WS1, WS1, D2 // WS2, WS2, c).transpose(0, 1, 3, 2, 4, 5).reshape(T, c)


def setup_inputs():
    n = np.random.standard_normal
    s = mx_kscale(T)
    u = mx_kscale(E)
    z0 = bf(n((B, NW, H, S, DH)) * 0.4)
    x = bf(n((B, E, D1, D2)))
    w0 = bf(n((E, E)) / np.sqrt(E))
    bo = bf(0.1 * n(E))
    g = n((B, D1, D2, E)) * np.exp2(np.random.randint(-6, 1, (B, D1, D2, 1))) * 4.0
    return {"z_heads": bf(f64(z0) * s.reshape(B, NW, 1, S, 1)),
            "x": x,
            "Wo": bf(f64(w0) / u),
            "bo": bo,
            "grad_out": bf(g / to_image(s.reshape(T, 1)) * u)}


def reference(z_heads, x, Wo, bo, grad_out):
    dp = to_windows(f64(grad_out))
    z = f64(z_heads).transpose(0, 1, 3, 2, 4).reshape(T, E)
    dz = mxq(dp, 1, "e5m2") @ mxq(f64(Wo), 1, "e4m3").T
    dw = mxq(z, 0, "e4m3").T @ mxq(dp, 0, "e5m2")
    dz_heads = dz.reshape(B, NW, S, H, DH).transpose(0, 1, 3, 2, 4)
    return dz_heads, dw

@@ -1,0 +1,230 @@
+from contextlib import ExitStack
+
+import concourse.mybir as mybir
+from concourse.masks import make_identity
+
+F32 = mybir.dt.float32
+BF16 = mybir.dt.bfloat16
+U32 = mybir.dt.uint32
+U8 = mybir.dt.uint8
+E4M3 = mybir.dt.float8_e4m3fn_x4
+E5M2 = mybir.dt.float8_e5m2_x4
+
+P = 128
+E = 1024
+FLOPS = 2 * 2 * E * E * E
+BYTES = 3 * 2 * E * E + 2 * 4 * E * E
+
+
+def tile_functatransformer_pb_v_kernel(tc, z_heads, x, Wo, bo, grad_out, out_0, out_1):
+    nc = tc.nc
+    with ExitStack() as ctx:
+        keep = ctx.enter_context(tc.tile_pool(name="keep", bufs=1))
+        psum = ctx.enter_context(tc.psum_pool(name="psum", bufs=4))
+        ctx.enter_context(tc.manual_schedule())
+
+        wo_raw = [keep.tile([P, 2, E], BF16, name=f"wo_raw{c}", align_bytes=64) for c in range(4)]
+        dp_raw = [keep.tile([P, 4, E], BF16, name=f"dp_raw{w}", align_bytes=64) for w in range(2)]
+        z_raw = [keep.tile([P, 32, 128], BF16, name=f"z_raw{w}", align_bytes=64) for w in range(2)]
+        ident = keep.tile([P, P], F32, name="ident", align_bytes=64)
+        perm = keep.tile([P, P], F32, name="perm", align_bytes=64)
+        zperm = keep.tile([P, P], BF16, name="zperm", align_bytes=64)
+        wo_g = [[keep.tile([P, 512 * 4], BF16, name=f"wo_g{g}{n}", align_bytes=64) for n in range(2)] for g in range(2)]
+        wo_c = [[keep.tile([P, 512], U32, name=f"wo_c{g}{n}", align_bytes=64) for n in range(2)] for g in range(2)]
+        wo_s = [[keep.tile([P, 512], U8, name=f"wo_s{g}{n}", align_bytes=64) for n in range(2)] for g in range(2)]
+        df_g = [[keep.tile([P, 512 * 4], BF16, name=f"df_g{g}{n}", align_bytes=64) for n in range(2)] for g in range(2)]
+        df_c = [[keep.tile([P, 512], U32, name=f"df_c{g}{n}", align_bytes=64) for n in range(2)] for g in range(2)]
+        df_s = [[keep.tile([P, 512], U8, name=f"df_s{g}{n}", align_bytes=64) for n in range(2)] for g in range(2)]
+        dt_g = [[keep.tile([P, 512 * 4], BF16, name=f"dt_g{w}{n}", align_bytes=64) for n in range(2)] for w in range(2)]
+        dt_c = [[keep.tile([P, 512], U32, name=f"dt_c{w}{n}", align_bytes=64) for n in range(2)] for w in range(2)]
+        dt_s = [[keep.tile([P, 512], U8, name=f"dt_s{w}{n}", align_bytes=64) for n in range(2)] for w in range(2)]
+        z_g = [[keep.tile([P, 512 * 4], BF16, name=f"z_g{w}{n}", align_bytes=64) for n in range(2)] for w in range(2)]
+        z_c = [[keep.tile([P, 512], U32, name=f"z_c{w}{n}", align_bytes=64) for n in range(2)] for w in range(2)]
+        z_s = [[keep.tile([P, 512], U8, name=f"z_s{w}{n}", align_bytes=64) for n in range(2)] for w in range(2)]
+        st0 = [keep.tile([P, 16, 8, 32], F32, name=f"st0_{n}", align_bytes=64) for n in range(2)]
+        st1 = [keep.tile([P, E], F32, name=f"st1_{m % 4}", align_bytes=64) for m in range(8)]
+
+        def load_wo(c):
+            nc.sync.dma_start(out=wo_raw[c][:], in_=Wo[256 * c : 256 * c + 256, :].rearrange("(n p) e -> p n e", p=P))
+
+        def load_dp(w):
+            rows = grad_out.rearrange("b i (q j) e -> (b i) q j e", j=4)
+            for hf in range(2):
+                q = (2 * w + hf + 1) % 4
+                nc.sync.dma_start(out=dp_raw[w][hf:P:2, :, :], in_=rows[:, q, :, :])
+
+        def load_z(w, bw):
+            b, wr = divmod(bw, 4)
+            nc.sync.dma_start(
+                out=z_raw[w][bw:P:8, :, :],
+                in_=z_heads[b, 2 * wr + w].rearrange("h (q j) d -> q h (j d)", j=4),
+            )
+
+        copy_on = {"s": nc.scalar.copy, "v": nc.vector.tensor_copy}
+
+        def wo_transposes(c, g, eng):
+            bank = psum.tile([P, 2, 256], F32, name="tr")
+            for n in range(2):
+                words = wo_raw[c][:, n, :].bitcast(F32)
+                for u in range(2):
+                    nc.tensor.transpose(bank[:, u, 128 * n : 128 * n + 128], words[:, 256 * g + u : 256 * g + 256 : 2], ident[:])
+            half, r = divmod(c, 2)
+            dst = wo_g[g][half][:].bitcast(F32).rearrange("p (c u) -> p c u", u=2)[:, 256 * r : 256 * r + 256, :]
+            copy_on[eng](out=dst, in_=bank[:].rearrange("p u c -> p c u"))
+
+        def dp_transposes(w, jp, g, eng):
+            bank = psum.tile([P, 2, 256], F32, name="tr")
+            for jj in range(2):
+                words = dp_raw[w][:, 2 * jp + jj, :].bitcast(F32)
+                for u in range(2):
+                    nc.tensor.transpose(bank[:, u, 128 * jj : 128 * jj + 128], words[:, 256 * g + u : 256 * g + 256 : 2], perm[:])
+            dst = df_g[g][jp][:].bitcast(F32).rearrange("p (x w c u) -> p x w c u", w=2, c=8, u=2)[:, :, w, :, :]
+            copy_on[eng](out=dst, in_=bank[:].rearrange("p u (x c) -> p x c u", c=8))
+
+        def quant(codes, scales, src, fmt):
+            nc.vector.quantize_mx(out=codes[:].bitcast(fmt), scales=scales[:], in_=src[:])
+
+        def out0_tile(jp, t, half, eng):
+            acc = psum.tile([P, 512], F32, name="mm")
+            for g in range(2):
+                nc.tensor.matmul_mx(
+                    out=acc[:],
+                    lhsT=df_c[g][jp][:, 128 * t : 128 * t + 128].bitcast(E5M2),
+                    lhsT_scale=df_s[g][jp][:, 128 * t : 128 * t + 128],
+                    rhs=wo_c[g][half][:].bitcast(E4M3),
+                    rhs_scale=wo_s[g][half][:],
+                    start=(g == 0),
+                    stop=(g == 1),
+                )
+            jj, hf = divmod(t, 2)
+            s8 = 4 * hf + 2 * jp + jj
+            copy_on[eng](out=st0[half][:, :, s8, :], in_=acc[:].rearrange("p (h d) -> p h d", d=32))
+
+        def store0(half):
+            for h in range(16):
+                view = out_0[:, :, 16 * half + h].rearrange("b w (s i) d -> (b w) s (i d)", i=8)
+                src = st0[half][:, h, :, :].rearrange("p i d -> p (i d)")
+                nc.sync.dma_start(out=view, in_=src)
+
+        def dt_interleave(w, n, k):
+            c0 = 512 * n + 256 * k
+            nc.vector.tensor_copy(
+                out=dt_g[w][n][:, 1024 * k : 1024 * k + 1024].rearrange("p (e j) -> p e j", j=4),
+                in_=dp_raw[w][:, :, c0 : c0 + 256].rearrange("p j e -> p e j"),
+            )
+
+        def z_chunk(w, k, eng):
+            bank = psum.tile([P, 2, 512], BF16, name="tr")
+            for i in range(2):
+                h0 = 8 * k + 4 * i
+                nc.tensor.matmul(
+                    bank[:, i, :], zperm[:], z_raw[w][:, h0 : h0 + 4, :].rearrange("p h x -> p (h x)"), start=True, stop=True
+                )
+            n, r = divmod(k, 2)
+            copy_on[eng](
+                out=z_g[w][n][:, 1024 * r : 1024 * r + 1024].rearrange("p (h d j) -> p h d j", h=8, j=4),
+                in_=bank[:].rearrange("p i (h j d) -> p (i h) d j", j=4, d=32),
+            )
+
+        def out1_tile(m, n, eng):
+            acc = psum.tile([P, 512], F32, name="mm")
+            nh, r = divmod(m, 4)
+            for w in range(2):
+                nc.tensor.matmul_mx(
+                    out=acc[:],
+                    lhsT=z_c[w][nh][:, 128 * r : 128 * r + 128].bitcast(E4M3),
+                    lhsT_scale=z_s[w][nh][:, 128 * r : 128 * r + 128],
+                    rhs=dt_c[w][n][:].bitcast(E5M2),
+                    rhs_scale=dt_s[w][n][:],
+                    start=(w == 0),
+                    stop=(w == 1),
+                )
+            copy_on[eng](out=st1[m][:, 512 * n : 512 * n + 512], in_=acc[:])
+
+        load_wo(0)
+        load_wo(1)
+        load_dp(0)
+        load_dp(1)
+        load_wo(2)
+        load_wo(3)
+        for w in range(2):
+            for bw in range(4):
+                load_z(w, bw)
+                load_z(w, bw + 4)
+        make_identity(nc, ident[:])
+        pv = perm[:].rearrange("p (hf b wr sh sl) -> p hf b wr sh sl", hf=2, b=2, wr=4, sh=2)
+        iv = ident[:].rearrange("p (b k m sl hf) -> p hf b k m sl", b=2, k=4, m=2, sl=4)
+        zv = zperm[:].rearrange("p (b k m sq) -> p b k m sq", b=2, k=4, m=2)
+        jv = ident[:].rearrange("p (sh sq b wr) -> p b wr sh sq", sh=2, sq=8, b=2)
+        for b in range(2):
+            nc.vector.tensor_copy(out=pv[:, :, b, :, 0, :], in_=iv[:, :, b, :, 1, :])
+            nc.vector.tensor_copy(out=pv[:, :, b, 0:3, 1, :], in_=iv[:, :, b, 1:4, 0, :])
+            nc.vector.tensor_copy(out=pv[:, :, b, 3, 1, :], in_=iv[:, :, b, 0, 0, :])
+        for b in range(2):
+            nc.vector.tensor_copy(out=zv[:, b, :, 1, :], in_=jv[:, b, :, 0, :])
+            nc.vector.tensor_copy(out=zv[:, b, 1:4, 0, :], in_=jv[:, b, 0:3, 1, :])
+            nc.vector.tensor_copy(out=zv[:, b, 0, 0, :], in_=jv[:, b, 3, 1, :])
+
+        for c in range(2):
+            wo_transposes(c, 0, "s")
+            wo_transposes(c, 1, "v")
+        quant(wo_c[0][0], wo_s[0][0], wo_g[0][0], E4M3)
+        quant(wo_c[1][0], wo_s[1][0], wo_g[1][0], E4M3)
+        dp_transposes(0, 0, 0, "s")
+        dp_transposes(0, 0, 1, "v")
+        dp_transposes(0, 1, 0, "s")
+        dp_transposes(0, 1, 1, "s")
+        dt_interleave(0, 0, 0)
+        dt_interleave(0, 0, 1)
+        dp_transposes(1, 0, 0, "s")
+        dp_transposes(1, 0, 1, "v")
+        dp_transposes(1, 1, 0, "s")
+        dp_transposes(1, 1, 1, "v")
+        quant(df_c[0][0], df_s[0][0], df_g[0][0], E5M2)
+        quant(df_c[1][0], df_s[1][0], df_g[1][0], E5M2)
+        wo_transposes(2, 0, "s")
+        wo_transposes(2, 1, "s")
+        quant(df_c[0][1], df_s[0][1], df_g[0][1], E5M2)
+        quant(df_c[1][1], df_s[1][1], df_g[1][1], E5M2)
+        wo_transposes(3, 0, "s")
+        wo_transposes(3, 1, "v")
+        for jp in range(2):
+            for t in range(4):
+                out0_tile(jp, t, 0, "s")
+        store0(0)
+        dt_interleave(0, 1, 0)
+        quant(wo_c[0][1], wo_s[0][1], wo_g[0][1], E4M3)
+        quant(wo_c[1][1], wo_s[1][1], wo_g[1][1], E4M3)
+        dt_interleave(0, 1, 1)
+        dt_interleave(1, 0, 0)
+        dt_interleave(1, 0, 1)
+        dt_interleave(1, 1, 0)
+        dt_interleave(1, 1, 1)
+        for jp in range(2):
+            for t in range(4):
+                out0_tile(jp, t, 1, "s")
+        store0(1)
+        for w in range(2):
+            for n in range(2):
+                quant(dt_c[w][n], dt_s[w][n], dt_g[w][n], E5M2)
+        z_chunk(0, 0, "v")
+        z_chunk(0, 1, "v")
+        z_chunk(0, 2, "v")
+        z_chunk(0, 3, "s")
+        z_chunk(1, 0, "v")
+        z_chunk(1, 1, "s")
+        quant(z_c[0][0], z_s[0][0], z_g[0][0], E4M3)
+        quant(z_c[1][0], z_s[1][0], z_g[1][0], E4M3)
+        z_chunk(1, 2, "v")
+        z_chunk(1, 3, "s")
+        for m in range(4):
+            out1_tile(m, 0, "s")
+            out1_tile(m, 1, "v")
+            nc.sync.dma_start(out=out_1[128 * m : 128 * m + 128, :], in_=st1[m][:])
+            if m == 0:
+                quant(z_c[0][1], z_s[0][1], z_g[0][1], E4M3)
+                quant(z_c[1][1], z_s[1][1], z_g[1][1], E4M3)
+        for m in range(4, 8):
+            out1_tile(m, 0, "s")
+            out1_tile(m, 1, "v")
+            nc.sync.dma_start(out=out_1[128 * m : 128 * m + 128, :], in_=st1[m][:])

@@ -20,126 +20,135 @@ def tile_functatransformer_pb_v_kernel(tc, z_heads, x, Wo, bo, grad_out, out_0, 
     nc = tc.nc
     with ExitStack() as ctx:
         keep = ctx.enter_context(tc.tile_pool(name="keep", bufs=1))
-        psum = ctx.enter_context(tc.psum_pool(name="psum", bufs=4))
+        psum = ctx.enter_context(tc.psum_pool(name="psum", bufs=8))
         ctx.enter_context(tc.manual_schedule())
 
+        def tiles(name, shape, dtype, n0, n1):
+            return [[keep.tile(shape, dtype, name=f"{name}{a}{b}", align_bytes=64) for b in range(n1)] for a in range(n0)]
+
         wo_raw = [keep.tile([P, 2, E], BF16, name=f"wo_raw{c}", align_bytes=64) for c in range(4)]
-        dp_raw = [keep.tile([P, 4, E], BF16, name=f"dp_raw{w}", align_bytes=64) for w in range(2)]
-        z_raw = [keep.tile([P, 32, 128], BF16, name=f"z_raw{w}", align_bytes=64) for w in range(2)]
+        dp_raw = [keep.tile([P, 2, 2 * E], BF16, name=f"dp_raw{w}", align_bytes=64) for w in range(2)]
+        dp_low = [keep.tile([P, 2 * E], BF16, name=f"dp_low{w}", align_bytes=64) for w in range(2)]
+        z_raw = keep.tile([P, 16 * 512], BF16, name="z_raw", align_bytes=64)
         ident = keep.tile([P, P], F32, name="ident", align_bytes=64)
+        ident_bf = keep.tile([P, P], BF16, name="ident_bf", align_bytes=64)
         perm = keep.tile([P, P], F32, name="perm", align_bytes=64)
-        zperm = keep.tile([P, P], BF16, name="zperm", align_bytes=64)
-        wo_g = [[keep.tile([P, 512 * 4], BF16, name=f"wo_g{g}{n}", align_bytes=64) for n in range(2)] for g in range(2)]
-        wo_c = [[keep.tile([P, 512], U32, name=f"wo_c{g}{n}", align_bytes=64) for n in range(2)] for g in range(2)]
-        wo_s = [[keep.tile([P, 512], U8, name=f"wo_s{g}{n}", align_bytes=64) for n in range(2)] for g in range(2)]
-        df_g = [[keep.tile([P, 512 * 4], BF16, name=f"df_g{g}{n}", align_bytes=64) for n in range(2)] for g in range(2)]
-        df_c = [[keep.tile([P, 512], U32, name=f"df_c{g}{n}", align_bytes=64) for n in range(2)] for g in range(2)]
-        df_s = [[keep.tile([P, 512], U8, name=f"df_s{g}{n}", align_bytes=64) for n in range(2)] for g in range(2)]
-        dt_g = [[keep.tile([P, 512 * 4], BF16, name=f"dt_g{w}{n}", align_bytes=64) for n in range(2)] for w in range(2)]
-        dt_c = [[keep.tile([P, 512], U32, name=f"dt_c{w}{n}", align_bytes=64) for n in range(2)] for w in range(2)]
-        dt_s = [[keep.tile([P, 512], U8, name=f"dt_s{w}{n}", align_bytes=64) for n in range(2)] for w in range(2)]
-        z_g = [[keep.tile([P, 512 * 4], BF16, name=f"z_g{w}{n}", align_bytes=64) for n in range(2)] for w in range(2)]
-        z_c = [[keep.tile([P, 512], U32, name=f"z_c{w}{n}", align_bytes=64) for n in range(2)] for w in range(2)]
-        z_s = [[keep.tile([P, 512], U8, name=f"z_s{w}{n}", align_bytes=64) for n in range(2)] for w in range(2)]
+        wo_g, wo_c, wo_s = tiles("wo_g", [P, 2048], BF16, 2, 2), tiles("wo_c", [P, 512], U32, 2, 2), tiles("wo_s", [P, 512], U8, 2, 2)
+        df_g = [keep.tile([P, 2, 2048], BF16, name=f"df_g{g}", align_bytes=64) for g in range(2)]
+        df_c, df_s = tiles("df_c", [P, 512], U32, 2, 2), tiles("df_s", [P, 512], U8, 2, 2)
+        dt_g, dt_c, dt_s = tiles("dt_g", [P, 2048], BF16, 2, 2), tiles("dt_c", [P, 512], U32, 2, 2), tiles("dt_s", [P, 512], U8, 2, 2)
+        z_g = [keep.tile([P, 1024], BF16, name=f"z_g{k}", align_bytes=64) for k in range(8)]
+        z_c = [keep.tile([P, 256], U32, name=f"z_c{k}", align_bytes=64) for k in range(8)]
+        z_s = [keep.tile([P, 256], U8, name=f"z_s{k}", align_bytes=64) for k in range(8)]
         st0 = [keep.tile([P, 16, 8, 32], F32, name=f"st0_{n}", align_bytes=64) for n in range(2)]
-        st1 = [keep.tile([P, E], F32, name=f"st1_{m % 4}", align_bytes=64) for m in range(8)]
+        st1 = [keep.tile([P, 2, E], F32, name=f"st1_{m}", align_bytes=64) for m in range(4)]
 
         def load_wo(c):
-            nc.sync.dma_start(out=wo_raw[c][:], in_=Wo[256 * c : 256 * c + 256, :].rearrange("(n p) e -> p n e", p=P))
+            nc.sync.dma_start(out=wo_raw[c][:], in_=Wo[256 * c : 256 * c + 256, :].rearrange("(p n) e -> p n e", n=2))
 
-        def load_dp(w):
-            rows = grad_out.rearrange("b i (q j) e -> (b i) q j e", j=4)
-            for hf in range(2):
-                q = (2 * w + hf + 1) % 4
-                nc.sync.dma_start(out=dp_raw[w][hf:P:2, :, :], in_=rows[:, q, :, :])
+        def dp_rows(wc, r1):
+            return dp_raw[wc][:, 0, :] if r1 == 0 else dp_low[wc][:]
 
-        def load_z(w, bw):
-            b, wr = divmod(bw, 4)
+        def load_dp(wc):
+            rows = grad_out.rearrange("b (ii r1 r0) (q c1 c0) e -> (b ii) r1 r0 q c1 (c0 e)", r1=2, r0=2, c1=2, c0=2)
+            for r1 in range(2):
+                for hf in range(2):
+                    q = (2 * wc + hf + 1) % 4
+                    for c1 in range(2):
+                        nc.sync.dma_start(out=dp_rows(wc, r1)[2 * hf + c1 : P : 4], in_=rows[:, r1, :, q, c1, :])
+
+        def load_z(b, wr, sh):
+            slot = 8 * b + (2 * wr + sh + 1) % 8
             nc.sync.dma_start(
-                out=z_raw[w][bw:P:8, :, :],
-                in_=z_heads[b, 2 * wr + w].rearrange("h (q j) d -> q h (j d)", j=4),
+                out=z_raw[:, 512 * slot : 512 * slot + 512],
+                in_=z_heads[b, 2 * wr : 2 * wr + 2, :, 32 * sh : 32 * sh + 32, :].rearrange("w h (r s) d -> (w h) r (s d)", r=2),
             )
 
         copy_on = {"s": nc.scalar.copy, "v": nc.vector.tensor_copy}
 
         def wo_transposes(c, g, eng):
-            bank = psum.tile([P, 2, 256], F32, name="tr")
+            bank = psum.tile([P, 2, 2, P], F32, name="bank")
             for n in range(2):
                 words = wo_raw[c][:, n, :].bitcast(F32)
                 for u in range(2):
-                    nc.tensor.transpose(bank[:, u, 128 * n : 128 * n + 128], words[:, 256 * g + u : 256 * g + 256 : 2], ident[:])
+                    nc.tensor.transpose(bank[:, u, n, :], words[:, 256 * g + u : 256 * g + 256 : 2], ident[:])
             half, r = divmod(c, 2)
-            dst = wo_g[g][half][:].bitcast(F32).rearrange("p (c u) -> p c u", u=2)[:, 256 * r : 256 * r + 256, :]
-            copy_on[eng](out=dst, in_=bank[:].rearrange("p u c -> p c u"))
+            dst = wo_g[g][half][:].bitcast(F32).rearrange("p (r q n u) -> p r q n u", r=2, n=2, u=2)[:, r]
+            copy_on[eng](out=dst, in_=bank[:].rearrange("p u n q -> p q n u"))
 
-        def dp_transposes(w, jp, g, eng):
-            bank = psum.tile([P, 2, 256], F32, name="tr")
-            for jj in range(2):
-                words = dp_raw[w][:, 2 * jp + jj, :].bitcast(F32)
+        def dp_transposes(wc, r1, g, eng):
+            bank = psum.tile([P, 2, 2, P], F32, name="bank")
+            for c0 in range(2):
+                words = dp_rows(wc, r1)[:, E * c0 : E * c0 + E].bitcast(F32)
                 for u in range(2):
-                    nc.tensor.transpose(bank[:, u, 128 * jj : 128 * jj + 128], words[:, 256 * g + u : 256 * g + 256 : 2], perm[:])
-            dst = df_g[g][jp][:].bitcast(F32).rearrange("p (x w c u) -> p x w c u", w=2, c=8, u=2)[:, :, w, :, :]
-            copy_on[eng](out=dst, in_=bank[:].rearrange("p u (x c) -> p x c u", c=8))
+                    nc.tensor.transpose(bank[:, u, c0, :], words[:, 256 * g + u : 256 * g + 256 : 2], perm[:])
+            dst = df_g[g][:].rearrange("p c n -> p (c n)").bitcast(F32)
+            dst = dst.rearrange("p (x w sh r1 r0 u) -> p x w sh r1 r0 u", w=2, sh=2, r1=2, r0=2, u=2)[:, :, wc, :, r1, :, :]
+            copy_on[eng](out=dst, in_=bank[:].rearrange("p u c (x sh r0) -> p (c x) sh r0 u", sh=2, r0=2))
+
+        def dp_join(wc):
+            nc.vector.tensor_copy(out=dp_raw[wc][:, 1, :], in_=dp_low[wc][:])
 
         def quant(codes, scales, src, fmt):
-            nc.vector.quantize_mx(out=codes[:].bitcast(fmt), scales=scales[:], in_=src[:])
+            nc.vector.quantize_mx(out=codes[:].bitcast(fmt), scales=scales[:], in_=src)
 
-        def out0_tile(jp, t, half, eng):
-            acc = psum.tile([P, 512], F32, name="mm")
+        def out0_pass(acc, col, half, g):
+            t, c0 = divmod(col, 2)
+            nc.tensor.matmul_mx(
+                out=acc[:],
+                lhsT=df_c[g][c0][:, 128 * t : 128 * t + 128].bitcast(E5M2),
+                lhsT_scale=df_s[g][c0][:, 128 * t : 128 * t + 128],
+                rhs=wo_c[g][half][:].bitcast(E4M3),
+                rhs_scale=wo_s[g][half][:],
+                start=(g == 0),
+                stop=(g == 1),
+            )
+
+        def out0_copy(acc, col, half, eng):
+            copy_on[eng](out=st0[half][:, :, col, :], in_=acc[:].rearrange("p (h d) -> p h d", d=32))
+
+        def out0_tile(col, half, eng):
+            acc = psum.tile([P, 512], F32, name="bank")
             for g in range(2):
-                nc.tensor.matmul_mx(
-                    out=acc[:],
-                    lhsT=df_c[g][jp][:, 128 * t : 128 * t + 128].bitcast(E5M2),
-                    lhsT_scale=df_s[g][jp][:, 128 * t : 128 * t + 128],
-                    rhs=wo_c[g][half][:].bitcast(E4M3),
-                    rhs_scale=wo_s[g][half][:],
-                    start=(g == 0),
-                    stop=(g == 1),
-                )
-            jj, hf = divmod(t, 2)
-            s8 = 4 * hf + 2 * jp + jj
-            copy_on[eng](out=st0[half][:, :, s8, :], in_=acc[:].rearrange("p (h d) -> p h d", d=32))
+                out0_pass(acc, col, half, g)
+            out0_copy(acc, col, half, eng)
 
         def store0(half):
             for h in range(16):
                 view = out_0[:, :, 16 * half + h].rearrange("b w (s i) d -> (b w) s (i d)", i=8)
-                src = st0[half][:, h, :, :].rearrange("p i d -> p (i d)")
-                nc.sync.dma_start(out=view, in_=src)
+                nc.sync.dma_start(out=view, in_=st0[half][:, h, :, :].rearrange("p i d -> p (i d)"))
 
-        def dt_interleave(w, n, k):
-            c0 = 512 * n + 256 * k
+        def dt_interleave(wc, n):
             nc.vector.tensor_copy(
-                out=dt_g[w][n][:, 1024 * k : 1024 * k + 1024].rearrange("p (e j) -> p e j", j=4),
-                in_=dp_raw[w][:, :, c0 : c0 + 256].rearrange("p j e -> p e j"),
+                out=dt_g[wc][n][:].rearrange("p (e c r) -> p e c r", c=2, r=2),
+                in_=dp_raw[wc][:].rearrange("p r (c e) -> p e c r", c=2)[:, 512 * n : 512 * n + 512],
             )
 
-        def z_chunk(w, k, eng):
-            bank = psum.tile([P, 2, 512], BF16, name="tr")
-            for i in range(2):
-                h0 = 8 * k + 4 * i
-                nc.tensor.matmul(
-                    bank[:, i, :], zperm[:], z_raw[w][:, h0 : h0 + 4, :].rearrange("p h x -> p (h x)"), start=True, stop=True
-                )
-            n, r = divmod(k, 2)
+        def z_bank():
+            return psum.tile([P, 4, 64, 2, 2], BF16, name="bank")
+
+        def z_turn(bank, k, dhi, c0):
+            first = 32 * c0 + 8 * dhi + k
+            nc.tensor.matmul(bank[:, dhi, :, c0, :], z_raw[:, first : 8192 : 64], ident_bf[:], start=True, stop=True)
+
+        def z_copy(bank, k, eng):
             copy_on[eng](
-                out=z_g[w][n][:, 1024 * r : 1024 * r + 1024].rearrange("p (h d j) -> p h d j", h=8, j=4),
-                in_=bank[:].rearrange("p i (h j d) -> p (i h) d j", j=4, d=32),
+                out=z_g[k][:].bitcast(F32).rearrange("p (x a w) -> p x a w", a=4, w=2),
+                in_=bank[:].rearrange("p a x c r -> p (a x c r)").bitcast(F32).rearrange("p (a x w) -> p x a w", a=4, w=2),
             )
 
-        def out1_tile(m, n, eng):
-            acc = psum.tile([P, 512], F32, name="mm")
-            nh, r = divmod(m, 4)
-            for w in range(2):
-                nc.tensor.matmul_mx(
-                    out=acc[:],
-                    lhsT=z_c[w][nh][:, 128 * r : 128 * r + 128].bitcast(E4M3),
-                    lhsT_scale=z_s[w][nh][:, 128 * r : 128 * r + 128],
-                    rhs=dt_c[w][n][:].bitcast(E5M2),
-                    rhs_scale=dt_s[w][n][:],
-                    start=(w == 0),
-                    stop=(w == 1),
-                )
-            copy_on[eng](out=st1[m][:, 512 * n : 512 * n + 512], in_=acc[:])
+        def out1_pass(acc, k, n, wc):
+            nc.tensor.matmul_mx(
+                out=acc[:],
+                lhsT=z_c[k][:, 128 * wc : 128 * wc + 128].bitcast(E4M3),
+                lhsT_scale=z_s[k][:, 128 * wc : 128 * wc + 128],
+                rhs=dt_c[wc][n][:].bitcast(E5M2),
+                rhs_scale=dt_s[wc][n][:],
+                start=(wc == 0),
+                stop=(wc == 1),
+            )
+
+        out1_rows = out_1.rearrange("(m k) e -> m k e", k=8)
 
         load_wo(0)
         load_wo(1)
@@ -147,84 +156,95 @@ def tile_functatransformer_pb_v_kernel(tc, z_heads, x, Wo, bo, grad_out, out_0, 
         load_dp(1)
         load_wo(2)
         load_wo(3)
-        for w in range(2):
-            for bw in range(4):
-                load_z(w, bw)
-                load_z(w, bw + 4)
+        for b in range(2):
+            for wr in range(4):
+                for sh in range(2):
+                    load_z(b, wr, sh)
+
         make_identity(nc, ident[:])
-        pv = perm[:].rearrange("p (hf b wr sh sl) -> p hf b wr sh sl", hf=2, b=2, wr=4, sh=2)
-        iv = ident[:].rearrange("p (b k m sl hf) -> p hf b k m sl", b=2, k=4, m=2, sl=4)
-        zv = zperm[:].rearrange("p (b k m sq) -> p b k m sq", b=2, k=4, m=2)
-        jv = ident[:].rearrange("p (sh sq b wr) -> p b wr sh sq", sh=2, sq=8, b=2)
+        pv = perm[:].rearrange("p (hc b wr sh r0) -> p hc b wr sh r0", hc=4, b=2, wr=4, sh=2)
+        iv = ident[:].rearrange("p (b k m r0 hc) -> p hc b k m r0", b=2, k=4, m=2, r0=2)
         for b in range(2):
             nc.vector.tensor_copy(out=pv[:, :, b, :, 0, :], in_=iv[:, :, b, :, 1, :])
             nc.vector.tensor_copy(out=pv[:, :, b, 0:3, 1, :], in_=iv[:, :, b, 1:4, 0, :])
             nc.vector.tensor_copy(out=pv[:, :, b, 3, 1, :], in_=iv[:, :, b, 0, 0, :])
-        for b in range(2):
-            nc.vector.tensor_copy(out=zv[:, b, :, 1, :], in_=jv[:, b, :, 0, :])
-            nc.vector.tensor_copy(out=zv[:, b, 1:4, 0, :], in_=jv[:, b, 0:3, 1, :])
-            nc.vector.tensor_copy(out=zv[:, b, 0, 0, :], in_=jv[:, b, 3, 1, :])
+        nc.vector.tensor_copy(out=ident_bf[:], in_=ident[:])
+
+        def q_wo(g, half):
+            quant(wo_c[g][half], wo_s[g][half], wo_g[g][half][:], E4M3)
+
+        def q_df(g, c0):
+            quant(df_c[g][c0], df_s[g][c0], df_g[g][:, c0, :], E5M2)
+
+        def q_dt(wc, n):
+            quant(dt_c[wc][n], dt_s[wc][n], dt_g[wc][n][:], E5M2)
+
+        def q_z(k):
+            quant(z_c[k], z_s[k], z_g[k][:], E4M3)
 
         for c in range(2):
             wo_transposes(c, 0, "s")
-            wo_transposes(c, 1, "v")
-        quant(wo_c[0][0], wo_s[0][0], wo_g[0][0], E4M3)
-        quant(wo_c[1][0], wo_s[1][0], wo_g[1][0], E4M3)
-        dp_transposes(0, 0, 0, "s")
-        dp_transposes(0, 0, 1, "v")
-        dp_transposes(0, 1, 0, "s")
-        dp_transposes(0, 1, 1, "s")
-        dt_interleave(0, 0, 0)
-        dt_interleave(0, 0, 1)
-        dp_transposes(1, 0, 0, "s")
-        dp_transposes(1, 0, 1, "v")
-        dp_transposes(1, 1, 0, "s")
-        dp_transposes(1, 1, 1, "v")
-        quant(df_c[0][0], df_s[0][0], df_g[0][0], E5M2)
-        quant(df_c[1][0], df_s[1][0], df_g[1][0], E5M2)
-        wo_transposes(2, 0, "s")
-        wo_transposes(2, 1, "s")
-        quant(df_c[0][1], df_s[0][1], df_g[0][1], E5M2)
-        quant(df_c[1][1], df_s[1][1], df_g[1][1], E5M2)
-        wo_transposes(3, 0, "s")
-        wo_transposes(3, 1, "v")
-        for jp in range(2):
-            for t in range(4):
-                out0_tile(jp, t, 0, "s")
+            wo_transposes(c, 1, "sv"[1 - c])
+        q_wo(0, 0)
+        q_wo(1, 0)
+        for r1 in range(2):
+            for g in range(2):
+                dp_transposes(0, r1, g, "s")
+        dp_join(0)
+        dt_interleave(0, 0)
+        dt_interleave(0, 1)
+        for r1 in range(2):
+            for g in range(2):
+                dp_transposes(1, r1, g, "s")
+        for c0 in range(2):
+            for g in range(2):
+                q_df(g, c0)
+        for c in range(2, 4):
+            for g in range(2):
+                wo_transposes(c, g, "s")
+        dp_join(1)
+        q_wo(0, 1)
+        q_wo(1, 1)
+        dt_interleave(1, 0)
+        for col in (0, 2, 4, 6, 1, 3, 5):
+            out0_tile(col, 0, "s")
+        out0_tile(7, 0, "v")
         store0(0)
-        dt_interleave(0, 1, 0)
-        quant(wo_c[0][1], wo_s[0][1], wo_g[0][1], E4M3)
-        quant(wo_c[1][1], wo_s[1][1], wo_g[1][1], E4M3)
-        dt_interleave(0, 1, 1)
-        dt_interleave(1, 0, 0)
-        dt_interleave(1, 0, 1)
-        dt_interleave(1, 1, 0)
-        dt_interleave(1, 1, 1)
-        for jp in range(2):
-            for t in range(4):
-                out0_tile(jp, t, 1, "s")
+        dt_interleave(1, 1)
+        q_dt(0, 0)
+        q_dt(1, 0)
+        for k in range(2):
+            bank = z_bank()
+            for dhi in range(4):
+                col = 4 * k + dhi
+                acc = psum.tile([P, 512], F32, name="bank")
+                for g in range(2):
+                    out0_pass(acc, col, 1, g)
+                    z_turn(bank, k, dhi, g)
+                out0_copy(acc, col, 1, "sssssssv"[col])
+            z_copy(bank, k, "vs"[k])
+            if k == 0:
+                q_dt(0, 1)
+                q_z(0)
+                q_dt(1, 1)
         store0(1)
-        for w in range(2):
+        for k in range(8):
+            ahead = k + 2
+            if ahead < 8:
+                bank = z_bank()
             for n in range(2):
-                quant(dt_c[w][n], dt_s[w][n], dt_g[w][n], E5M2)
-        z_chunk(0, 0, "v")
-        z_chunk(0, 1, "v")
-        z_chunk(0, 2, "v")
-        z_chunk(0, 3, "s")
-        z_chunk(1, 0, "v")
-        z_chunk(1, 1, "s")
-        quant(z_c[0][0], z_s[0][0], z_g[0][0], E4M3)
-        quant(z_c[1][0], z_s[1][0], z_g[1][0], E4M3)
-        z_chunk(1, 2, "v")
-        z_chunk(1, 3, "s")
-        for m in range(4):
-            out1_tile(m, 0, "s")
-            out1_tile(m, 1, "v")
-            nc.sync.dma_start(out=out_1[128 * m : 128 * m + 128, :], in_=st1[m][:])
-            if m == 0:
-                quant(z_c[0][1], z_s[0][1], z_g[0][1], E4M3)
-                quant(z_c[1][1], z_s[1][1], z_g[1][1], E4M3)
-        for m in range(4, 8):
-            out1_tile(m, 0, "s")
-            out1_tile(m, 1, "v")
-            nc.sync.dma_start(out=out_1[128 * m : 128 * m + 128, :], in_=st1[m][:])
+                acc = psum.tile([P, 512], F32, name="bank")
+                for wc in range(2):
+                    out1_pass(acc, k, n, wc)
+                    if ahead < 8:
+                        z_turn(bank, ahead, 2 * n + wc, 0)
+                        z_turn(bank, ahead, 2 * n + wc, 1)
+                if n == 0 and k + 1 < 8:
+                    q_z(k + 1)
+                copy_on["sv"[n]](out=st1[k // 2][:, k % 2, 512 * n : 512 * n + 512], in_=acc[:])
+            if ahead < 8:
+                z_copy(bank, ahead, "s")
+            if k >= 4:
+                nc.sync.dma_start(out=out1_rows[:, k, :], in_=st1[k // 2][:, k % 2, :])
+            elif k % 2 == 1:
+                nc.sync.dma_start(out=out1_rows[:, k - 1 : k + 1, :], in_=st1[k // 2][:])

@@ -30,6 +30,7 @@ def tile_functatransformer_pb_v_kernel(tc, z_heads, x, Wo, bo, grad_out, out_0, 
         dp_raw = [keep.tile([P, 2, 2 * E], BF16, name=f"dp_raw{w}", align_bytes=64) for w in range(2)]
         dp_low = [keep.tile([P, 2 * E], BF16, name=f"dp_low{w}", align_bytes=64) for w in range(2)]
         z_raw = keep.tile([P, 16 * 512], BF16, name="z_raw", align_bytes=64)
+        z_srt = [keep.tile([P, 4, 2, 256], BF16, name=f"z_srt{a}", align_bytes=64) for a in range(4)]
         ident = keep.tile([P, P], F32, name="ident", align_bytes=64)
         ident_bf = keep.tile([P, P], BF16, name="ident_bf", align_bytes=64)
         perm = keep.tile([P, P], F32, name="perm", align_bytes=64)
@@ -37,7 +38,7 @@ def tile_functatransformer_pb_v_kernel(tc, z_heads, x, Wo, bo, grad_out, out_0, 
         df_g = [keep.tile([P, 2, 2048], BF16, name=f"df_g{g}", align_bytes=64) for g in range(2)]
         df_c, df_s = tiles("df_c", [P, 512], U32, 2, 2), tiles("df_s", [P, 512], U8, 2, 2)
         dt_g, dt_c, dt_s = tiles("dt_g", [P, 2048], BF16, 2, 2), tiles("dt_c", [P, 512], U32, 2, 2), tiles("dt_s", [P, 512], U8, 2, 2)
-        z_g = [keep.tile([P, 1024], BF16, name=f"z_g{k}", align_bytes=64) for k in range(8)]
+        z_g = [keep.tile([P, 1024], BF16, name=f"z_g{k % 4}", align_bytes=64) for k in range(8)]
         z_c = [keep.tile([P, 256], U32, name=f"z_c{k}", align_bytes=64) for k in range(8)]
         z_s = [keep.tile([P, 256], U8, name=f"z_s{k}", align_bytes=64) for k in range(8)]
         st0 = [keep.tile([P, 16, 8, 32], F32, name=f"st0_{n}", align_bytes=64) for n in range(2)]
@@ -128,8 +129,20 @@ def tile_functatransformer_pb_v_kernel(tc, z_heads, x, Wo, bo, grad_out, out_0, 
             return psum.tile([P, 4, 64, 2, 2], BF16, name="bank")
 
         def z_turn(bank, k, dhi, c0):
-            first = 32 * c0 + 8 * dhi + k
-            nc.tensor.matmul(bank[:, dhi, :, c0, :], z_raw[:, first : 8192 : 64], ident_bf[:], start=True, stop=True)
+            nc.tensor.matmul(bank[:, dhi, :, c0, :], z_srt[k // 2][:, dhi, c0, k % 2 : 256 : 2], ident_bf[:], start=True, stop=True)
+
+        def z_sort(a):
+            nc.vector.tensor_copy(
+                out=z_srt[a][:].rearrange("p a c n -> p (a c n)").bitcast(F32).rearrange("p (a c j) -> p a c j", a=4, c=2),
+                in_=z_raw[:].bitcast(F32).rearrange("p (j c a w) -> p a c j w", c=2, a=4, w=4)[:, :, :, :, a],
+            )
+
+        def z_tile(k, eng):
+            bank = z_bank()
+            for dhi in range(4):
+                for c0 in range(2):
+                    z_turn(bank, k, dhi, c0)
+            z_copy(bank, k, eng)
 
         def z_copy(bank, k, eng):
             copy_on[eng](
@@ -150,12 +163,10 @@ def tile_functatransformer_pb_v_kernel(tc, z_heads, x, Wo, bo, grad_out, out_0, 
 
         out1_rows = out_1.rearrange("(m k) e -> m k e", k=8)
 
-        load_wo(0)
-        load_wo(1)
         load_dp(0)
         load_dp(1)
-        load_wo(2)
-        load_wo(3)
+        for c in range(4):
+            load_wo(c)
         for b in range(2):
             for wr in range(4):
                 for sh in range(2):
@@ -182,68 +193,59 @@ def tile_functatransformer_pb_v_kernel(tc, z_heads, x, Wo, bo, grad_out, out_0, 
         def q_z(k):
             quant(z_c[k], z_s[k], z_g[k][:], E4M3)
 
-        for c in range(2):
-            wo_transposes(c, 0, "s")
-            wo_transposes(c, 1, "sv"[1 - c])
-        q_wo(0, 0)
-        q_wo(1, 0)
-        for r1 in range(2):
-            for g in range(2):
-                dp_transposes(0, r1, g, "s")
-        dp_join(0)
-        dt_interleave(0, 0)
-        dt_interleave(0, 1)
-        for r1 in range(2):
-            for g in range(2):
-                dp_transposes(1, r1, g, "s")
-        for c0 in range(2):
-            for g in range(2):
-                q_df(g, c0)
-        for c in range(2, 4):
+        for wc in range(2):
+            for r1 in range(2):
+                for g in range(2):
+                    dp_transposes(wc, r1, g, "svssssss"[4 * wc + 2 * r1 + g])
+            dp_join(wc)
+            if wc == 0:
+                dt_interleave(0, 0)
+                dt_interleave(0, 1)
+        for c in range(4):
             for g in range(2):
                 wo_transposes(c, g, "s")
-        dp_join(1)
+            if c == 0:
+                q_df(0, 0)
+                q_df(1, 0)
+                q_df(0, 1)
+            if c == 1:
+                q_wo(0, 0)
+                q_wo(1, 0)
+        q_df(1, 1)
+        dt_interleave(1, 0)
+        dt_interleave(1, 1)
         q_wo(0, 1)
         q_wo(1, 1)
-        dt_interleave(1, 0)
-        for col in (0, 2, 4, 6, 1, 3, 5):
-            out0_tile(col, 0, "s")
-        out0_tile(7, 0, "v")
-        store0(0)
-        dt_interleave(1, 1)
         q_dt(0, 0)
         q_dt(1, 0)
-        for k in range(2):
-            bank = z_bank()
-            for dhi in range(4):
-                col = 4 * k + dhi
-                acc = psum.tile([P, 512], F32, name="bank")
-                for g in range(2):
-                    out0_pass(acc, col, 1, g)
-                    z_turn(bank, k, dhi, g)
-                out0_copy(acc, col, 1, "sssssssv"[col])
-            z_copy(bank, k, "vs"[k])
-            if k == 0:
-                q_dt(0, 1)
-                q_z(0)
-                q_dt(1, 1)
+        for col, eng in zip((0, 2, 4, 6, 1, 3, 5, 7), "sssssssv"):
+            out0_tile(col, 0, eng)
+        store0(0)
+        z_sort(0)
+        q_dt(0, 1)
+        for col in range(4):
+            out0_tile(col, 1, "sssvsssv"[col])
+        z_tile(0, "v")
+        q_dt(1, 1)
+        q_z(0)
+        z_sort(1)
+        for col in range(4, 8):
+            out0_tile(col, 1, "sssvsssv"[col])
         store0(1)
+        z_tile(1, "s")
+        q_z(1)
         for k in range(8):
-            ahead = k + 2
-            if ahead < 8:
-                bank = z_bank()
             for n in range(2):
                 acc = psum.tile([P, 512], F32, name="bank")
                 for wc in range(2):
                     out1_pass(acc, k, n, wc)
-                    if ahead < 8:
-                        z_turn(bank, ahead, 2 * n + wc, 0)
-                        z_turn(bank, ahead, 2 * n + wc, 1)
-                if n == 0 and k + 1 < 8:
-                    q_z(k + 1)
                 copy_on["sv"[n]](out=st1[k // 2][:, k % 2, 512 * n : 512 * n + 512], in_=acc[:])
-            if ahead < 8:
-                z_copy(bank, ahead, "s")
+                if n == 0 and k + 2 < 8:
+                    z_tile(k + 2, "s")
+            if k + 2 < 8:
+                q_z(k + 2)
+            if k in (0, 2):
+                z_sort(k // 2 + 2)
             if k >= 4:
                 nc.sync.dma_start(out=out1_rows[:, k, :], in_=st1[k // 2][:, k % 2, :])
             elif k % 2 == 1:

@@ -12,6 +12,7 @@ E5M2 = mybir.dt.float8_e5m2_x4
 
 P = 128
 E = 1024
+AHEAD = 3
 FLOPS = 2 * 2 * E * E * E
 BYTES = 3 * 2 * E * E + 2 * 4 * E * E
 
@@ -30,7 +31,7 @@ def tile_functatransformer_pb_v_kernel(tc, z_heads, x, Wo, bo, grad_out, out_0, 
         dp_raw = [keep.tile([P, 2, 2 * E], BF16, name=f"dp_raw{w}", align_bytes=64) for w in range(2)]
         dp_low = [keep.tile([P, 2 * E], BF16, name=f"dp_low{w}", align_bytes=64) for w in range(2)]
         z_raw = keep.tile([P, 16 * 512], BF16, name="z_raw", align_bytes=64)
-        z_srt = [keep.tile([P, 4, 2, 256], BF16, name=f"z_srt{a}", align_bytes=64) for a in range(4)]
+        z_srt = [keep.tile([P, 2, 8, 256], BF16, name=f"z_srt{a}", align_bytes=64) for a in range(2)]
         ident = keep.tile([P, P], F32, name="ident", align_bytes=64)
         ident_bf = keep.tile([P, P], BF16, name="ident_bf", align_bytes=64)
         perm = keep.tile([P, P], F32, name="perm", align_bytes=64)
@@ -125,29 +126,19 @@ def tile_functatransformer_pb_v_kernel(tc, z_heads, x, Wo, bo, grad_out, out_0, 
                 in_=dp_raw[wc][:].rearrange("p r (c e) -> p e c r", c=2)[:, 512 * n : 512 * n + 512],
             )
 
-        def z_bank():
-            return psum.tile([P, 4, 64, 2, 2], BF16, name="bank")
-
-        def z_turn(bank, k, dhi, c0):
-            nc.tensor.matmul(bank[:, dhi, :, c0, :], z_srt[k // 2][:, dhi, c0, k % 2 : 256 : 2], ident_bf[:], start=True, stop=True)
-
-        def z_sort(a):
-            nc.vector.tensor_copy(
-                out=z_srt[a][:].rearrange("p a c n -> p (a c n)").bitcast(F32).rearrange("p (a c j) -> p a c j", a=4, c=2),
-                in_=z_raw[:].bitcast(F32).rearrange("p (j c a w) -> p a c j w", c=2, a=4, w=4)[:, :, :, :, a],
-            )
+        def z_sort(a, c0):
+            src = z_raw[:].bitcast(F32).rearrange("p (j c dhi a w) -> p c a dhi j w", c=2, dhi=4, a=2, w=2)
+            dst = z_srt[a][:].rearrange("p w m n -> p (w m n)").bitcast(F32).rearrange("p (w dhi c j) -> p c dhi j w", w=2, dhi=4, c=2)
+            nc.vector.tensor_copy(out=dst[:, c0], in_=src[:, c0, a])
 
         def z_tile(k, eng):
-            bank = z_bank()
-            for dhi in range(4):
-                for c0 in range(2):
-                    z_turn(bank, k, dhi, c0)
-            z_copy(bank, k, eng)
-
-        def z_copy(bank, k, eng):
+            a, w, e = k // 4, k // 2 % 2, k % 2
+            bank = psum.tile([P, 8, P], BF16, name="bank")
+            for m in range(8):
+                nc.tensor.matmul(bank[:, m, :], z_srt[a][:, w, m, e : 256 : 2], ident_bf[:], start=True, stop=True)
             copy_on[eng](
-                out=z_g[k][:].bitcast(F32).rearrange("p (x a w) -> p x a w", a=4, w=2),
-                in_=bank[:].rearrange("p a x c r -> p (a x c r)").bitcast(F32).rearrange("p (a x w) -> p x a w", a=4, w=2),
+                out=z_g[k][:].bitcast(F32).rearrange("p (x m) -> p x m", m=8),
+                in_=bank[:].rearrange("p m n -> p (m n)").bitcast(F32).rearrange("p (m x) -> p x m", m=8),
             )
 
         def out1_pass(acc, k, n, wc):
@@ -217,36 +208,39 @@ def tile_functatransformer_pb_v_kernel(tc, z_heads, x, Wo, bo, grad_out, out_0, 
         q_wo(0, 1)
         q_wo(1, 1)
         q_dt(0, 0)
-        q_dt(1, 0)
-        for col, eng in zip((0, 2, 4, 6, 1, 3, 5, 7), "sssssssv"):
+        for col, eng in zip((0, 2, 4, 6, 1, 3, 5, 7), "ssssssss"):
             out0_tile(col, 0, eng)
         store0(0)
-        z_sort(0)
-        q_dt(0, 1)
-        for col in range(4):
-            out0_tile(col, 1, "sssvsssv"[col])
-        z_tile(0, "v")
-        q_dt(1, 1)
-        q_z(0)
-        z_sort(1)
-        for col in range(4, 8):
-            out0_tile(col, 1, "sssvsssv"[col])
+        z_sort(0, 0)
+        z_sort(0, 1)
+        q_dt(1, 0)
+        for col in range(8):
+            out0_tile(col, 1, "s")
+            if col == 4:
+                z_tile(0, "v")
         store0(1)
+        q_dt(0, 1)
+        q_z(0)
+        q_dt(1, 1)
         z_tile(1, "s")
+        z_sort(1, 0)
         q_z(1)
+        z_sort(1, 1)
+        for k in range(2, AHEAD):
+            z_tile(k, "s")
+            q_z(k)
         for k in range(8):
             for n in range(2):
                 acc = psum.tile([P, 512], F32, name="bank")
                 for wc in range(2):
                     out1_pass(acc, k, n, wc)
                 copy_on["sv"[n]](out=st1[k // 2][:, k % 2, 512 * n : 512 * n + 512], in_=acc[:])
-                if n == 0 and k + 2 < 8:
-                    z_tile(k + 2, "s")
-            if k + 2 < 8:
-                q_z(k + 2)
-            if k in (0, 2):
-                z_sort(k // 2 + 2)
-            if k >= 4:
+                if n == 0 and k + AHEAD < 8:
+                    z_tile(k + AHEAD, "s")
+                    q_z(k + AHEAD)
+                if k == 7:
+                    nc.sync.dma_start(out=out1_rows[:, k, 512 * n : 512 * n + 512], in_=st1[3][:, 1, 512 * n : 512 * n + 512])
+            if 2 <= k < 7:
                 nc.sync.dma_start(out=out1_rows[:, k, :], in_=st1[k // 2][:, k % 2, :])
-            elif k % 2 == 1:
+            elif k == 1:
                 nc.sync.dma_start(out=out1_rows[:, k - 1 : k + 1, :], in_=st1[k // 2][:])

@@ -12,7 +12,6 @@ E5M2 = mybir.dt.float8_e5m2_x4
 
 P = 128
 E = 1024
-AHEAD = 3
 FLOPS = 2 * 2 * E * E * E
 BYTES = 3 * 2 * E * E + 2 * 4 * E * E
 
@@ -33,15 +32,14 @@ def tile_functatransformer_pb_v_kernel(tc, z_heads, x, Wo, bo, grad_out, out_0, 
         z_raw = keep.tile([P, 16 * 512], BF16, name="z_raw", align_bytes=64)
         z_srt = [keep.tile([P, 2, 8, 256], BF16, name=f"z_srt{a}", align_bytes=64) for a in range(2)]
         ident = keep.tile([P, P], F32, name="ident", align_bytes=64)
-        ident_bf = keep.tile([P, P], BF16, name="ident_bf", align_bytes=64)
         perm = keep.tile([P, P], F32, name="perm", align_bytes=64)
         wo_g, wo_c, wo_s = tiles("wo_g", [P, 2048], BF16, 2, 2), tiles("wo_c", [P, 512], U32, 2, 2), tiles("wo_s", [P, 512], U8, 2, 2)
         df_g = [keep.tile([P, 2, 2048], BF16, name=f"df_g{g}", align_bytes=64) for g in range(2)]
         df_c, df_s = tiles("df_c", [P, 512], U32, 2, 2), tiles("df_s", [P, 512], U8, 2, 2)
         dt_g, dt_c, dt_s = tiles("dt_g", [P, 2048], BF16, 2, 2), tiles("dt_c", [P, 512], U32, 2, 2), tiles("dt_s", [P, 512], U8, 2, 2)
-        z_g = [keep.tile([P, 1024], BF16, name=f"z_g{k % 4}", align_bytes=64) for k in range(8)]
-        z_c = [keep.tile([P, 256], U32, name=f"z_c{k}", align_bytes=64) for k in range(8)]
-        z_s = [keep.tile([P, 256], U8, name=f"z_s{k}", align_bytes=64) for k in range(8)]
+        z_g = [keep.tile([P, 2048], BF16, name=f"z_g{k % 2}", align_bytes=64) for k in range(4)]
+        z_c = [keep.tile([P, 512], U32, name=f"z_c{k}", align_bytes=64) for k in range(4)]
+        z_s = [keep.tile([P, 512], U8, name=f"z_s{k}", align_bytes=64) for k in range(4)]
         st0 = [keep.tile([P, 16, 8, 32], F32, name=f"st0_{n}", align_bytes=64) for n in range(2)]
         st1 = [keep.tile([P, 2, E], F32, name=f"st1_{m}", align_bytes=64) for m in range(4)]
 
@@ -94,29 +92,25 @@ def tile_functatransformer_pb_v_kernel(tc, z_heads, x, Wo, bo, grad_out, out_0, 
         def quant(codes, scales, src, fmt):
             nc.vector.quantize_mx(out=codes[:].bitcast(fmt), scales=scales[:], in_=src)
 
-        def out0_pass(acc, col, half, g):
-            t, c0 = divmod(col, 2)
-            nc.tensor.matmul_mx(
-                out=acc[:],
-                lhsT=df_c[g][c0][:, 128 * t : 128 * t + 128].bitcast(E5M2),
-                lhsT_scale=df_s[g][c0][:, 128 * t : 128 * t + 128],
-                rhs=wo_c[g][half][:].bitcast(E4M3),
-                rhs_scale=wo_s[g][half][:],
-                start=(g == 0),
-                stop=(g == 1),
-            )
+        def out0_pair(t, c0, quarter, eng):
+            half, r = divmod(quarter, 2)
+            acc = psum.tile([P, 2, 256], F32, name="bank")
+            for i in range(2):
+                for g in range(2):
+                    nc.tensor.matmul_mx(
+                        out=acc[:, i, :],
+                        lhsT=df_c[g][c0][:, 128 * (t + i) : 128 * (t + i) + 128].bitcast(E5M2),
+                        lhsT_scale=df_s[g][c0][:, 128 * (t + i) : 128 * (t + i) + 128],
+                        rhs=wo_c[g][half][:, 256 * r : 256 * r + 256].bitcast(E4M3),
+                        rhs_scale=wo_s[g][half][:, 256 * r : 256 * r + 256],
+                        start=(g == 0),
+                        stop=(g == 1),
+                    )
+            dst = st0[half][:, 8 * r : 8 * r + 8].rearrange("p h (t c) d -> p h t c d", c=2)[:, :, t : t + 2, c0, :]
+            copy_on[eng](out=dst, in_=acc[:].rearrange("p i (h d) -> p h i d", d=32))
 
-        def out0_copy(acc, col, half, eng):
-            copy_on[eng](out=st0[half][:, :, col, :], in_=acc[:].rearrange("p (h d) -> p h d", d=32))
-
-        def out0_tile(col, half, eng):
-            acc = psum.tile([P, 512], F32, name="bank")
-            for g in range(2):
-                out0_pass(acc, col, half, g)
-            out0_copy(acc, col, half, eng)
-
-        def store0(half):
-            for h in range(16):
+        def store0(half, heads):
+            for h in heads:
                 view = out_0[:, :, 16 * half + h].rearrange("b w (s i) d -> (b w) s (i d)", i=8)
                 nc.sync.dma_start(out=view, in_=st0[half][:, h, :, :].rearrange("p i d -> p (i d)"))
 
@@ -131,21 +125,22 @@ def tile_functatransformer_pb_v_kernel(tc, z_heads, x, Wo, bo, grad_out, out_0, 
             dst = z_srt[a][:].rearrange("p w m n -> p (w m n)").bitcast(F32).rearrange("p (w dhi c j) -> p c dhi j w", w=2, dhi=4, c=2)
             nc.vector.tensor_copy(out=dst[:, c0], in_=src[:, c0, a])
 
-        def z_tile(k, eng):
-            a, w, e = k // 4, k // 2 % 2, k % 2
-            bank = psum.tile([P, 8, P], BF16, name="bank")
-            for m in range(8):
-                nc.tensor.matmul(bank[:, m, :], z_srt[a][:, w, m, e : 256 : 2], ident_bf[:], start=True, stop=True)
-            copy_on[eng](
-                out=z_g[k][:].bitcast(F32).rearrange("p (x m) -> p x m", m=8),
-                in_=bank[:].rearrange("p m n -> p (m n)").bitcast(F32).rearrange("p (m x) -> p x m", m=8),
-            )
+        def z_pair(kp, engs):
+            a, w = divmod(kp, 2)
+            words = z_srt[a][:, w].rearrange("p m n -> p (m n)").bitcast(F32)
+            dst = z_g[kp][:].rearrange("p (e x u m r) -> p u e x m r", e=2, u=2, m=4, r=2)
+            for u in range(2):
+                bank = psum.tile([P, 4, P], F32, name="bank")
+                for m in range(4):
+                    nc.tensor.transpose(bank[:, m, :], words[:, 128 * (4 * u + m) : 128 * (4 * u + m) + 128], ident[:])
+                src = bank[:].rearrange("p m n -> p (m n)").bitcast(BF16).rearrange("p (m x r e) -> p e x m r", m=4, r=2, e=2)
+                copy_on[engs[u]](out=dst[:, u], in_=src)
 
         def out1_pass(acc, k, n, wc):
             nc.tensor.matmul_mx(
                 out=acc[:],
-                lhsT=z_c[k][:, 128 * wc : 128 * wc + 128].bitcast(E4M3),
-                lhsT_scale=z_s[k][:, 128 * wc : 128 * wc + 128],
+                lhsT=z_c[k // 2][:, 256 * (k % 2) + 128 * wc : 256 * (k % 2) + 128 * wc + 128].bitcast(E4M3),
+                lhsT_scale=z_s[k // 2][:, 256 * (k % 2) + 128 * wc : 256 * (k % 2) + 128 * wc + 128],
                 rhs=dt_c[wc][n][:].bitcast(E5M2),
                 rhs_scale=dt_s[wc][n][:],
                 start=(wc == 0),
@@ -170,10 +165,28 @@ def tile_functatransformer_pb_v_kernel(tc, z_heads, x, Wo, bo, grad_out, out_0, 
             nc.vector.tensor_copy(out=pv[:, :, b, :, 0, :], in_=iv[:, :, b, :, 1, :])
             nc.vector.tensor_copy(out=pv[:, :, b, 0:3, 1, :], in_=iv[:, :, b, 1:4, 0, :])
             nc.vector.tensor_copy(out=pv[:, :, b, 3, 1, :], in_=iv[:, :, b, 0, 0, :])
-        nc.vector.tensor_copy(out=ident_bf[:], in_=ident[:])
 
-        def q_wo(g, half):
-            quant(wo_c[g][half], wo_s[g][half], wo_g[g][half][:], E4M3)
+        def q_wo_quarter(g, quarter):
+            half, r = divmod(quarter, 2)
+            nc.vector.quantize_mx(
+                out=wo_c[g][half][:, 256 * r : 256 * r + 256].bitcast(E4M3),
+                scales=wo_s[g][half][:, 256 * r : 256 * r + 256],
+                in_=wo_g[g][half][:, 1024 * r : 1024 * r + 1024],
+            )
+
+        def out0_quarter(quarter, engs):
+            for i, (c0, t) in enumerate(((0, 0), (0, 2), (1, 0), (1, 2))):
+                out0_pair(t, c0, quarter, engs[i])
+            store0(quarter // 2, range(8 * (quarter % 2), 8 * (quarter % 2) + 8))
+
+        def out1_half(k, n, eng):
+            acc = psum.tile([P, 512], F32, name="bank")
+            for wc in range(2):
+                out1_pass(acc, k, n, wc)
+            copy_on[eng](out=st1[k // 2][:, k % 2, 512 * n : 512 * n + 512], in_=acc[:])
+
+        def store1(k, lo, hi):
+            nc.sync.dma_start(out=out1_rows[:, k, lo:hi], in_=st1[k // 2][:, k % 2, lo:hi])
 
         def q_df(g, c0):
             quant(df_c[g][c0], df_s[g][c0], df_g[g][:, c0, :], E5M2)
@@ -188,59 +201,56 @@ def tile_functatransformer_pb_v_kernel(tc, z_heads, x, Wo, bo, grad_out, out_0, 
             for r1 in range(2):
                 for g in range(2):
                     dp_transposes(wc, r1, g, "svssssss"[4 * wc + 2 * r1 + g])
-            dp_join(wc)
             if wc == 0:
+                dp_join(0)
                 dt_interleave(0, 0)
                 dt_interleave(0, 1)
-        for c in range(4):
+        for c in range(3):
             for g in range(2):
                 wo_transposes(c, g, "s")
             if c == 0:
                 q_df(0, 0)
                 q_df(1, 0)
+                q_wo_quarter(0, 0)
+                q_wo_quarter(1, 0)
                 q_df(0, 1)
+                q_df(1, 1)
             if c == 1:
-                q_wo(0, 0)
-                q_wo(1, 0)
-        q_df(1, 1)
+                dp_join(1)
+                q_wo_quarter(0, 1)
+                q_wo_quarter(1, 1)
+        q_wo_quarter(0, 2)
+        q_wo_quarter(1, 2)
         dt_interleave(1, 0)
         dt_interleave(1, 1)
-        q_wo(0, 1)
-        q_wo(1, 1)
+        out0_quarter(0, "ssss")
+        out0_quarter(1, "ssss")
         q_dt(0, 0)
-        for col, eng in zip((0, 2, 4, 6, 1, 3, 5, 7), "ssssssss"):
-            out0_tile(col, 0, eng)
-        store0(0)
         z_sort(0, 0)
         z_sort(0, 1)
+        for g in range(2):
+            wo_transposes(3, g, "s")
+        q_wo_quarter(0, 3)
+        q_wo_quarter(1, 3)
         q_dt(1, 0)
-        for col in range(8):
-            out0_tile(col, 1, "s")
-            if col == 4:
-                z_tile(0, "v")
-        store0(1)
         q_dt(0, 1)
-        q_z(0)
         q_dt(1, 1)
-        z_tile(1, "s")
+        out0_quarter(2, "ssss")
+        z_pair(0, "vs")
         z_sort(1, 0)
-        q_z(1)
+        q_z(0)
         z_sort(1, 1)
-        for k in range(2, AHEAD):
-            z_tile(k, "s")
-            q_z(k)
+        out0_quarter(3, "sssv")
+        z_pair(1, "sv")
+        q_z(1)
         for k in range(8):
             for n in range(2):
-                acc = psum.tile([P, 512], F32, name="bank")
-                for wc in range(2):
-                    out1_pass(acc, k, n, wc)
-                copy_on["sv"[n]](out=st1[k // 2][:, k % 2, 512 * n : 512 * n + 512], in_=acc[:])
-                if n == 0 and k + AHEAD < 8:
-                    z_tile(k + AHEAD, "s")
-                    q_z(k + AHEAD)
-                if k == 7:
-                    nc.sync.dma_start(out=out1_rows[:, k, 512 * n : 512 * n + 512], in_=st1[3][:, 1, 512 * n : 512 * n + 512])
-            if 2 <= k < 7:
-                nc.sync.dma_start(out=out1_rows[:, k, :], in_=st1[k // 2][:, k % 2, :])
-            elif k == 1:
-                nc.sync.dma_start(out=out1_rows[:, k - 1 : k + 1, :], in_=st1[k // 2][:])
+                out1_half(k, n, "ssvsvsvsvsvsvsvs"[2 * k + n])
+                if k >= 7:
+                    store1(k, 512 * n, 512 * n + 512)
+            if k < 7:
+                store1(k, 0, E)
+            if k in (0, 2):
+                z_pair(k // 2 + 2, "sv")
+            if k in (1, 3):
+                q_z(k // 2 + 2)

@@ -32,12 +32,13 @@ def tile_functatransformer_pb_v_kernel(tc, z_heads, x, Wo, bo, grad_out, out_0, 
         z_raw = keep.tile([P, 16 * 512], BF16, name="z_raw", align_bytes=64)
         z_srt = [keep.tile([P, 2, 8, 256], BF16, name=f"z_srt{a}", align_bytes=64) for a in range(2)]
         ident = keep.tile([P, P], F32, name="ident", align_bytes=64)
+        ident_bf = keep.tile([P, P], BF16, name="ident_bf", align_bytes=64)
         perm = keep.tile([P, P], F32, name="perm", align_bytes=64)
         wo_g, wo_c, wo_s = tiles("wo_g", [P, 2048], BF16, 2, 2), tiles("wo_c", [P, 512], U32, 2, 2), tiles("wo_s", [P, 512], U8, 2, 2)
         df_g = [keep.tile([P, 2, 2048], BF16, name=f"df_g{g}", align_bytes=64) for g in range(2)]
         df_c, df_s = tiles("df_c", [P, 512], U32, 2, 2), tiles("df_s", [P, 512], U8, 2, 2)
         dt_g, dt_c, dt_s = tiles("dt_g", [P, 2048], BF16, 2, 2), tiles("dt_c", [P, 512], U32, 2, 2), tiles("dt_s", [P, 512], U8, 2, 2)
-        z_g = [keep.tile([P, 2048], BF16, name=f"z_g{k % 2}", align_bytes=64) for k in range(4)]
+        z_g = [keep.tile([P, 1024], BF16, name=f"z_g{k % 4}", align_bytes=64) for k in range(8)]
         z_c = [keep.tile([P, 512], U32, name=f"z_c{k}", align_bytes=64) for k in range(4)]
         z_s = [keep.tile([P, 512], U8, name=f"z_s{k}", align_bytes=64) for k in range(4)]
         st0 = [keep.tile([P, 16, 8, 32], F32, name=f"st0_{n}", align_bytes=64) for n in range(2)]
@@ -125,16 +126,15 @@ def tile_functatransformer_pb_v_kernel(tc, z_heads, x, Wo, bo, grad_out, out_0, 
             dst = z_srt[a][:].rearrange("p w m n -> p (w m n)").bitcast(F32).rearrange("p (w dhi c j) -> p c dhi j w", w=2, dhi=4, c=2)
             nc.vector.tensor_copy(out=dst[:, c0], in_=src[:, c0, a])
 
-        def z_pair(kp, engs):
-            a, w = divmod(kp, 2)
-            words = z_srt[a][:, w].rearrange("p m n -> p (m n)").bitcast(F32)
-            dst = z_g[kp][:].rearrange("p (e x u m r) -> p u e x m r", e=2, u=2, m=4, r=2)
-            for u in range(2):
-                bank = psum.tile([P, 4, P], F32, name="bank")
-                for m in range(4):
-                    nc.tensor.transpose(bank[:, m, :], words[:, 128 * (4 * u + m) : 128 * (4 * u + m) + 128], ident[:])
-                src = bank[:].rearrange("p m n -> p (m n)").bitcast(BF16).rearrange("p (m x r e) -> p e x m r", m=4, r=2, e=2)
-                copy_on[engs[u]](out=dst[:, u], in_=src)
+        def z_tile(k, eng):
+            a, w, e = k // 4, k // 2 % 2, k % 2
+            bank = psum.tile([P, 8, P], BF16, name="bank")
+            for m in range(8):
+                nc.tensor.matmul(bank[:, m, :], z_srt[a][:, w, m, e : 256 : 2], ident_bf[:], start=True, stop=True)
+            copy_on[eng](
+                out=z_g[k][:].bitcast(F32).rearrange("p (x m) -> p x m", m=8),
+                in_=bank[:].rearrange("p m n -> p (m n)").bitcast(F32).rearrange("p (m x) -> p x m", m=8),
+            )
 
         def out1_pass(acc, k, n, wc):
             nc.tensor.matmul_mx(
@@ -165,6 +165,7 @@ def tile_functatransformer_pb_v_kernel(tc, z_heads, x, Wo, bo, grad_out, out_0, 
             nc.vector.tensor_copy(out=pv[:, :, b, :, 0, :], in_=iv[:, :, b, :, 1, :])
             nc.vector.tensor_copy(out=pv[:, :, b, 0:3, 1, :], in_=iv[:, :, b, 1:4, 0, :])
             nc.vector.tensor_copy(out=pv[:, :, b, 3, 1, :], in_=iv[:, :, b, 0, 0, :])
+        nc.vector.tensor_copy(out=ident_bf[:], in_=ident[:])
 
         def q_wo_quarter(g, quarter):
             half, r = divmod(quarter, 2)
@@ -172,6 +173,14 @@ def tile_functatransformer_pb_v_kernel(tc, z_heads, x, Wo, bo, grad_out, out_0, 
                 out=wo_c[g][half][:, 256 * r : 256 * r + 256].bitcast(E4M3),
                 scales=wo_s[g][half][:, 256 * r : 256 * r + 256],
                 in_=wo_g[g][half][:, 1024 * r : 1024 * r + 1024],
+            )
+
+        def q_z_tile(k):
+            kp, e = divmod(k, 2)
+            nc.vector.quantize_mx(
+                out=z_c[kp][:, 256 * e : 256 * e + 256].bitcast(E4M3),
+                scales=z_s[kp][:, 256 * e : 256 * e + 256],
+                in_=z_g[k][:],
             )
 
         def out0_quarter(quarter, engs):
@@ -193,9 +202,6 @@ def tile_functatransformer_pb_v_kernel(tc, z_heads, x, Wo, bo, grad_out, out_0, 
 
         def q_dt(wc, n):
             quant(dt_c[wc][n], dt_s[wc][n], dt_g[wc][n][:], E5M2)
-
-        def q_z(k):
-            quant(z_c[k], z_s[k], z_g[k][:], E4M3)
 
         for wc in range(2):
             for r1 in range(2):
@@ -236,21 +242,23 @@ def tile_functatransformer_pb_v_kernel(tc, z_heads, x, Wo, bo, grad_out, out_0, 
         q_dt(0, 1)
         q_dt(1, 1)
         out0_quarter(2, "ssss")
-        z_pair(0, "vs")
+        z_tile(0, "v")
+        z_tile(1, "v")
         z_sort(1, 0)
-        q_z(0)
+        q_z_tile(0)
+        q_z_tile(1)
         z_sort(1, 1)
-        out0_quarter(3, "sssv")
-        z_pair(1, "sv")
-        q_z(1)
+        out0_quarter(3, "ssss")
+        z_tile(2, "v")
+        q_z_tile(2)
         for k in range(8):
             for n in range(2):
-                out1_half(k, n, "ssvsvsvsvsvsvsvs"[2 * k + n])
+                out1_half(k, n, "sv"[n])
+                if n == 0 and k + 3 < 8:
+                    z_tile(k + 3, "s")
                 if k >= 7:
                     store1(k, 512 * n, 512 * n + 512)
+            if k + 3 < 8:
+                q_z_tile(k + 3)
             if k < 7:
                 store1(k, 0, E)
-            if k in (0, 2):
-                z_pair(k // 2 + 2, "sv")
-            if k in (1, 3):
-                q_z(k // 2 + 2)

@@ -38,14 +38,14 @@ def tile_functatransformer_pb_v_kernel(tc, z_heads, x, Wo, bo, grad_out, out_0, 
         df_g = [keep.tile([P, 2, 2048], BF16, name=f"df_g{g}", align_bytes=64) for g in range(2)]
         df_c, df_s = tiles("df_c", [P, 512], U32, 2, 2), tiles("df_s", [P, 512], U8, 2, 2)
         dt_g, dt_c, dt_s = tiles("dt_g", [P, 2048], BF16, 2, 2), tiles("dt_c", [P, 512], U32, 2, 2), tiles("dt_s", [P, 512], U8, 2, 2)
-        z_g = [keep.tile([P, 1024], BF16, name=f"z_g{k % 4}", align_bytes=64) for k in range(8)]
+        z_g = [keep.tile([P, 2048], BF16, name=f"z_g{k % 2}", align_bytes=64) for k in range(4)]
         z_c = [keep.tile([P, 512], U32, name=f"z_c{k}", align_bytes=64) for k in range(4)]
         z_s = [keep.tile([P, 512], U8, name=f"z_s{k}", align_bytes=64) for k in range(4)]
         st0 = [keep.tile([P, 16, 8, 32], F32, name=f"st0_{n}", align_bytes=64) for n in range(2)]
         st1 = [keep.tile([P, 2, E], F32, name=f"st1_{m}", align_bytes=64) for m in range(4)]
 
         def load_wo(c):
-            nc.sync.dma_start(out=wo_raw[c][:], in_=Wo[256 * c : 256 * c + 256, :].rearrange("(p n) e -> p n e", n=2))
+            nc.sync.dma_start(out=wo_raw[c][:], in_=Wo[256 * c : 256 * c + 256, :].rearrange("(n p) e -> p n e", n=2))
 
         def dp_rows(wc, r1):
             return dp_raw[wc][:, 0, :] if r1 == 0 else dp_low[wc][:]
@@ -74,8 +74,8 @@ def tile_functatransformer_pb_v_kernel(tc, z_heads, x, Wo, bo, grad_out, out_0, 
                 for u in range(2):
                     nc.tensor.transpose(bank[:, u, n, :], words[:, 256 * g + u : 256 * g + 256 : 2], ident[:])
             half, r = divmod(c, 2)
-            dst = wo_g[g][half][:].bitcast(F32).rearrange("p (r q n u) -> p r q n u", r=2, n=2, u=2)[:, r]
-            copy_on[eng](out=dst, in_=bank[:].rearrange("p u n q -> p q n u"))
+            dst = wo_g[g][half][:].bitcast(F32).rearrange("p (r n q u) -> p r n q u", r=2, n=2, u=2)[:, r]
+            copy_on[eng](out=dst, in_=bank[:].rearrange("p u n q -> p n q u"))
 
         def dp_transposes(wc, r1, g, eng):
             bank = psum.tile([P, 2, 2, P], F32, name="bank")
@@ -132,8 +132,8 @@ def tile_functatransformer_pb_v_kernel(tc, z_heads, x, Wo, bo, grad_out, out_0, 
             for m in range(8):
                 nc.tensor.matmul(bank[:, m, :], z_srt[a][:, w, m, e : 256 : 2], ident_bf[:], start=True, stop=True)
             copy_on[eng](
-                out=z_g[k][:].bitcast(F32).rearrange("p (x m) -> p x m", m=8),
-                in_=bank[:].rearrange("p m n -> p (m n)").bitcast(F32).rearrange("p (m x) -> p x m", m=8),
+                out=z_g[k // 2][:, 1024 * e : 1024 * e + 1024].bitcast(F32).rearrange("p (x u m) -> p u x m", u=2, m=4),
+                in_=bank[:].rearrange("p m n -> p (m n)").bitcast(F32).rearrange("p (u m x) -> p u x m", u=2, m=4),
             )
 
         def out1_pass(acc, k, n, wc):
@@ -175,14 +175,6 @@ def tile_functatransformer_pb_v_kernel(tc, z_heads, x, Wo, bo, grad_out, out_0, 
                 in_=wo_g[g][half][:, 1024 * r : 1024 * r + 1024],
             )
 
-        def q_z_tile(k):
-            kp, e = divmod(k, 2)
-            nc.vector.quantize_mx(
-                out=z_c[kp][:, 256 * e : 256 * e + 256].bitcast(E4M3),
-                scales=z_s[kp][:, 256 * e : 256 * e + 256],
-                in_=z_g[k][:],
-            )
-
         def out0_quarter(quarter, engs):
             for i, (c0, t) in enumerate(((0, 0), (0, 2), (1, 0), (1, 2))):
                 out0_pair(t, c0, quarter, engs[i])
@@ -202,6 +194,9 @@ def tile_functatransformer_pb_v_kernel(tc, z_heads, x, Wo, bo, grad_out, out_0, 
 
         def q_dt(wc, n):
             quant(dt_c[wc][n], dt_s[wc][n], dt_g[wc][n][:], E5M2)
+
+        def q_z(k):
+            quant(z_c[k], z_s[k], z_g[k][:], E4M3)
 
         for wc in range(2):
             for r1 in range(2):
@@ -242,23 +237,24 @@ def tile_functatransformer_pb_v_kernel(tc, z_heads, x, Wo, bo, grad_out, out_0, 
         q_dt(0, 1)
         q_dt(1, 1)
         out0_quarter(2, "ssss")
-        z_tile(0, "v")
+        z_tile(0, "s")
         z_tile(1, "v")
         z_sort(1, 0)
-        q_z_tile(0)
-        q_z_tile(1)
+        q_z(0)
         z_sort(1, 1)
         out0_quarter(3, "ssss")
         z_tile(2, "v")
-        q_z_tile(2)
+        z_tile(3, "s")
+        q_z(1)
         for k in range(8):
             for n in range(2):
-                out1_half(k, n, "sv"[n])
-                if n == 0 and k + 3 < 8:
-                    z_tile(k + 3, "s")
+                out1_half(k, n, "ssvsvsvsvsvsvsvs"[2 * k + n])
                 if k >= 7:
                     store1(k, 512 * n, 512 * n + 512)
-            if k + 3 < 8:
-                q_z_tile(k + 3)
             if k < 7:
                 store1(k, 0, E)
+            if k in (0, 2):
+                z_tile(k + 4, "s")
+                z_tile(k + 5, "v")
+            if k in (1, 3):
+                q_z(k // 2 + 2)

@@ -27,8 +27,9 @@ def tile_functatransformer_pb_v_kernel(tc, z_heads, x, Wo, bo, grad_out, out_0, 
             return [[keep.tile(shape, dtype, name=f"{name}{a}{b}", align_bytes=64) for b in range(n1)] for a in range(n0)]
 
         wo_raw = [keep.tile([P, 2, E], BF16, name=f"wo_raw{c}", align_bytes=64) for c in range(4)]
+        wo_srt = {}
         dp_raw = [keep.tile([P, 2, 2 * E], BF16, name=f"dp_raw{w}", align_bytes=64) for w in range(2)]
-        dp_low = [keep.tile([P, 2 * E], BF16, name=f"dp_low{w}", align_bytes=64) for w in range(2)]
+        dp_low = [keep.tile([P, 2 * E], BF16, name="spare", bufs=2, align_bytes=64) for w in range(2)]
         z_raw = keep.tile([P, 16 * 512], BF16, name="z_raw", align_bytes=64)
         z_srt = [keep.tile([P, 2, 8, 256], BF16, name=f"z_srt{a}", align_bytes=64) for a in range(2)]
         ident = keep.tile([P, P], F32, name="ident", align_bytes=64)
@@ -70,12 +71,22 @@ def tile_functatransformer_pb_v_kernel(tc, z_heads, x, Wo, bo, grad_out, out_0, 
         def wo_transposes(c, g, eng):
             bank = psum.tile([P, 2, 2, P], F32, name="bank")
             for n in range(2):
-                words = wo_raw[c][:, n, :].bitcast(F32)
                 for u in range(2):
-                    nc.tensor.transpose(bank[:, u, n, :], words[:, 256 * g + u : 256 * g + 256 : 2], ident[:])
+                    if c < 2:
+                        words = wo_raw[c][:, n, :].bitcast(F32)[:, 256 * g + u : 256 * g + 256 : 2]
+                    else:
+                        words = wo_srt[c][:].rearrange("p (n g u j) -> p n g u j", n=2, g=2, u=2)[:, n, g, u, :]
+                    nc.tensor.transpose(bank[:, u, n, :], words, ident[:])
             half, r = divmod(c, 2)
             dst = wo_g[g][half][:].bitcast(F32).rearrange("p (r n q u) -> p r n q u", r=2, n=2, u=2)[:, r]
             copy_on[eng](out=dst, in_=bank[:].rearrange("p u n q -> p n q u"))
+
+        def wo_sort(c):
+            wo_srt[c] = keep.tile([P, 2 * 2 * 2 * P], F32, name="spare", bufs=2, align_bytes=64)
+            nc.vector.tensor_copy(
+                out=wo_srt[c][:].rearrange("p (m u j) -> p m u j", u=2, j=P),
+                in_=wo_raw[c][:].rearrange("p n e -> p (n e)").bitcast(F32).rearrange("p (m j u) -> p m u j", u=2, j=P),
+            )
 
         def dp_transposes(wc, r1, g, eng):
             bank = psum.tile([P, 2, 2, P], F32, name="bank")
@@ -88,7 +99,10 @@ def tile_functatransformer_pb_v_kernel(tc, z_heads, x, Wo, bo, grad_out, out_0, 
             copy_on[eng](out=dst, in_=bank[:].rearrange("p u c (x sh r0) -> p (c x) sh r0 u", sh=2, r0=2))
 
         def dp_join(wc):
-            nc.vector.tensor_copy(out=dp_raw[wc][:, 1, :], in_=dp_low[wc][:])
+            dst = dp_raw[wc][:, 1, :].rearrange("p (c n e) -> p n c e", c=2, n=2)
+            src = dp_low[wc][:].rearrange("p (c n e) -> p n c e", c=2, n=2)
+            for n in range(2):
+                nc.vector.tensor_copy(out=dst[:, n], in_=src[:, n])
 
         def quant(codes, scales, src, fmt):
             nc.vector.quantize_mx(out=codes[:].bitcast(fmt), scales=scales[:], in_=src)
@@ -201,12 +215,12 @@ def tile_functatransformer_pb_v_kernel(tc, z_heads, x, Wo, bo, grad_out, out_0, 
         for wc in range(2):
             for r1 in range(2):
                 for g in range(2):
-                    dp_transposes(wc, r1, g, "svssssss"[4 * wc + 2 * r1 + g])
+                    dp_transposes(wc, r1, g, "ssssssss"[4 * wc + 2 * r1 + g])
+            dp_join(wc)
             if wc == 0:
-                dp_join(0)
                 dt_interleave(0, 0)
                 dt_interleave(0, 1)
-        for c in range(3):
+        for c in range(2):
             for g in range(2):
                 wo_transposes(c, g, "s")
             if c == 0:
@@ -216,45 +230,46 @@ def tile_functatransformer_pb_v_kernel(tc, z_heads, x, Wo, bo, grad_out, out_0, 
                 q_wo_quarter(1, 0)
                 q_df(0, 1)
                 q_df(1, 1)
-            if c == 1:
-                dp_join(1)
-                q_wo_quarter(0, 1)
-                q_wo_quarter(1, 1)
+        wo_sort(2)
+        wo_sort(3)
+        q_wo_quarter(0, 1)
+        q_wo_quarter(1, 1)
+        out0_quarter(0, "ssss")
+        dt_interleave(1, 0)
+        for c in range(2, 4):
+            for g in range(2):
+                wo_transposes(c, g, "sssv"[2 * c + g - 4])
+        q_dt(0, 0)
         q_wo_quarter(0, 2)
         q_wo_quarter(1, 2)
-        dt_interleave(1, 0)
-        dt_interleave(1, 1)
-        out0_quarter(0, "ssss")
-        out0_quarter(1, "ssss")
-        q_dt(0, 0)
-        z_sort(0, 0)
-        z_sort(0, 1)
-        for g in range(2):
-            wo_transposes(3, g, "s")
+        q_dt(1, 0)
         q_wo_quarter(0, 3)
         q_wo_quarter(1, 3)
-        q_dt(1, 0)
-        q_dt(0, 1)
-        q_dt(1, 1)
+        out0_quarter(1, "ssss")
+        z_sort(0, 0)
+        z_sort(0, 1)
         out0_quarter(2, "ssss")
-        z_tile(0, "s")
-        z_tile(1, "v")
-        z_sort(1, 0)
+        dt_interleave(1, 1)
+        z_tile(0, "v")
+        z_tile(1, "s")
+        q_dt(0, 1)
         q_z(0)
-        z_sort(1, 1)
         out0_quarter(3, "ssss")
+        q_dt(1, 1)
+        z_sort(1, 0)
         z_tile(2, "v")
         z_tile(3, "s")
+        z_sort(1, 1)
         q_z(1)
         for k in range(8):
             for n in range(2):
-                out1_half(k, n, "ssvsvsvsvsvsvsvs"[2 * k + n])
+                out1_half(k, n, "ssvsvssvvssvsvsv"[2 * k + n])
+                if k in (2, 4) and n == 0:
+                    q_z(k // 2 + 1)
                 if k >= 7:
                     store1(k, 512 * n, 512 * n + 512)
             if k < 7:
                 store1(k, 0, E)
-            if k in (0, 2):
-                z_tile(k + 4, "s")
-                z_tile(k + 5, "v")
             if k in (1, 3):
-                q_z(k // 2 + 2)
+                z_tile(k + 3, "v")
+                z_tile(k + 4, "s")

@@ -127,7 +127,7 @@ def tile_functatransformer_pb_v_kernel(tc, z_heads, x, Wo, bo, grad_out, out_0, 
         def store0(half, heads):
             for h in heads:
                 view = out_0[:, :, 16 * half + h].rearrange("b w (s i) d -> (b w) s (i d)", i=8)
-                nc.sync.dma_start(out=view, in_=st0[half][:, h, :, :].rearrange("p i d -> p (i d)"))
+                nc.sync.dma_start(out=view, in_=st0[half][:, h, :, :].rearrange("p i d -> p (i d)"), max_dma_last_dim=1024)
 
         def dt_interleave(wc, n):
             nc.vector.tensor_copy(

@@ -95,8 +95,8 @@ def tile_functatransformer_pb_v_kernel(tc, z_heads, x, Wo, bo, grad_out, out_0, 
                 for u in range(2):
                     nc.tensor.transpose(bank[:, u, c0, :], words[:, 256 * g + u : 256 * g + 256 : 2], perm[:])
             dst = df_g[g][:].rearrange("p c n -> p (c n)").bitcast(F32)
-            dst = dst.rearrange("p (x w sh r1 r0 u) -> p x w sh r1 r0 u", w=2, sh=2, r1=2, r0=2, u=2)[:, :, wc, :, r1, :, :]
-            copy_on[eng](out=dst, in_=bank[:].rearrange("p u c (x sh r0) -> p (c x) sh r0 u", sh=2, r0=2))
+            dst = dst.rearrange("p (x w r1 r0 u) -> p x w r1 r0 u", w=2, r1=2, r0=2, u=2)[:, :, wc, r1, :, :]
+            copy_on[eng](out=dst, in_=bank[:].rearrange("p u c (x r0) -> p (c x) r0 u", r0=2))
 
         def dp_join(wc):
             dst = dp_raw[wc][:, 1, :].rearrange("p (c n e) -> p n c e", c=2, n=2)
@@ -124,10 +124,12 @@ def tile_functatransformer_pb_v_kernel(tc, z_heads, x, Wo, bo, grad_out, out_0, 
             dst = st0[half][:, 8 * r : 8 * r + 8].rearrange("p h (t c) d -> p h t c d", c=2)[:, :, t : t + 2, c0, :]
             copy_on[eng](out=dst, in_=acc[:].rearrange("p i (h d) -> p h i d", d=32))
 
-        def store0(half, heads):
-            for h in heads:
-                view = out_0[:, :, 16 * half + h].rearrange("b w (s i) d -> (b w) s (i d)", i=8)
-                nc.sync.dma_start(out=view, in_=st0[half][:, h, :, :].rearrange("p i d -> p (i d)"), max_dma_last_dim=1024)
+        def store0(quarter, s, sh, lo=0, hi=16):
+            half, r = divmod(quarter, 2)
+            view = out_0[:, :, 8 * quarter : 8 * quarter + 8].rearrange("b w h (sh s i) d -> sh s (b w) h (i d)", sh=2, i=8)
+            first = 64 * sh + s
+            src = st0[half][first + 4 * lo : first + 4 * hi - 3 : 4, 8 * r : 8 * r + 8]
+            nc.sync.dma_start(out=view[sh, s, lo:hi], in_=src.rearrange("p h i d -> p h (i d)"))
 
         def dt_interleave(wc, n):
             nc.vector.tensor_copy(
@@ -173,7 +175,7 @@ def tile_functatransformer_pb_v_kernel(tc, z_heads, x, Wo, bo, grad_out, out_0, 
                     load_z(b, wr, sh)
 
         make_identity(nc, ident[:])
-        pv = perm[:].rearrange("p (hc b wr sh r0) -> p hc b wr sh r0", hc=4, b=2, wr=4, sh=2)
+        pv = perm[:].rearrange("p (hc sh b wr r0) -> p hc b wr sh r0", hc=4, b=2, wr=4, sh=2)
         iv = ident[:].rearrange("p (b k m r0 hc) -> p hc b k m r0", b=2, k=4, m=2, r0=2)
         for b in range(2):
             nc.vector.tensor_copy(out=pv[:, :, b, :, 0, :], in_=iv[:, :, b, :, 1, :])
@@ -189,10 +191,20 @@ def tile_functatransformer_pb_v_kernel(tc, z_heads, x, Wo, bo, grad_out, out_0, 
                 in_=wo_g[g][half][:, 1024 * r : 1024 * r + 1024],
             )
 
+        def out0_banks(quarter, banks, engs):
+            for i, eng in zip(banks, engs):
+                out0_pair(2 * (i % 2), i // 2, quarter, eng)
+
+        def out0_stores(quarter):
+            for s in range(4):
+                for sh in (1, 0):
+                    store0(quarter, s, sh, hi=8 if (quarter, s, sh) == (0, 0, 0) else 16)
+            if quarter == 3:
+                store0(0, 0, 0, lo=8)
+
         def out0_quarter(quarter, engs):
-            for i, (c0, t) in enumerate(((0, 0), (0, 2), (1, 0), (1, 2))):
-                out0_pair(t, c0, quarter, engs[i])
-            store0(quarter // 2, range(8 * (quarter % 2), 8 * (quarter % 2) + 8))
+            out0_banks(quarter, range(4), engs)
+            out0_stores(quarter)
 
         def out1_half(k, n, eng):
             acc = psum.tile([P, 512], F32, name="bank")
@@ -234,42 +246,46 @@ def tile_functatransformer_pb_v_kernel(tc, z_heads, x, Wo, bo, grad_out, out_0, 
         wo_sort(3)
         q_wo_quarter(0, 1)
         q_wo_quarter(1, 1)
-        out0_quarter(0, "ssss")
+        out0_banks(0, range(3), "sss")
         dt_interleave(1, 0)
         for c in range(2, 4):
             for g in range(2):
-                wo_transposes(c, g, "sssv"[2 * c + g - 4])
-        q_dt(0, 0)
+                wo_transposes(c, g, "svsv"[2 * c + g - 4])
         q_wo_quarter(0, 2)
         q_wo_quarter(1, 2)
-        q_dt(1, 0)
         q_wo_quarter(0, 3)
         q_wo_quarter(1, 3)
+        out0_banks(0, range(3, 4), "s")
+        out0_stores(0)
         out0_quarter(1, "ssss")
+        q_dt(0, 0)
+        q_dt(1, 0)
         z_sort(0, 0)
         z_sort(0, 1)
         out0_quarter(2, "ssss")
         dt_interleave(1, 1)
+        z_sort(1, 0)
+        z_sort(1, 1)
+        out0_quarter(3, "ssss")
         z_tile(0, "v")
         z_tile(1, "s")
         q_dt(0, 1)
         q_z(0)
-        out0_quarter(3, "ssss")
-        q_dt(1, 1)
-        z_sort(1, 0)
-        z_tile(2, "v")
+        z_tile(2, "s")
         z_tile(3, "s")
-        z_sort(1, 1)
+        q_dt(1, 1)
         q_z(1)
+        z_tile(4, "v")
+        z_tile(5, "s")
         for k in range(8):
             for n in range(2):
-                out1_half(k, n, "ssvsvssvvssvsvsv"[2 * k + n])
-                if k in (2, 4) and n == 0:
-                    q_z(k // 2 + 1)
+                out1_half(k, n, "vssvsvsvvssvsvsv"[2 * k + n])
+                if k in (0, 4) and n == 0:
+                    q_z(k // 4 + 2)
                 if k >= 7:
                     store1(k, 512 * n, 512 * n + 512)
             if k < 7:
                 store1(k, 0, E)
-            if k in (1, 3):
-                z_tile(k + 3, "v")
-                z_tile(k + 4, "s")
+            if k == 3:
+                z_tile(6, "v")
+                z_tile(7, "s")

@@ -30,7 +30,7 @@ def tile_functatransformer_pb_v_kernel(tc, z_heads, x, Wo, bo, grad_out, out_0, 
         wo_srt = {}
         dp_raw = [keep.tile([P, 2, 2 * E], BF16, name=f"dp_raw{w}", align_bytes=64) for w in range(2)]
         dp_low = [keep.tile([P, 2 * E], BF16, name="spare", bufs=2, align_bytes=64) for w in range(2)]
-        z_raw = keep.tile([P, 16 * 512], BF16, name="z_raw", align_bytes=64)
+        z_raw = keep.tile([P, 17 * 512], BF16, name="z_raw", align_bytes=64)
         z_srt = [keep.tile([P, 2, 8, 256], BF16, name=f"z_srt{a}", align_bytes=64) for a in range(2)]
         ident = keep.tile([P, P], F32, name="ident", align_bytes=64)
         ident_bf = keep.tile([P, P], BF16, name="ident_bf", align_bytes=64)
@@ -52,19 +52,21 @@ def tile_functatransformer_pb_v_kernel(tc, z_heads, x, Wo, bo, grad_out, out_0, 
             return dp_raw[wc][:, 0, :] if r1 == 0 else dp_low[wc][:]
 
         def load_dp(wc):
-            rows = grad_out.rearrange("b (ii r1 r0) (q c1 c0) e -> (b ii) r1 r0 q c1 (c0 e)", r1=2, r0=2, c1=2, c0=2)
+            rows = grad_out.rearrange("b (ii r1 r0) (q c1 c0) e -> (b ii r1) r0 q c1 (c0 e)", r1=2, r0=2, c1=2, c0=2)
+            pairs = grad_out.rearrange("b (i r0) (c c0) e -> (b i) r0 c (c0 e)", r0=2, c0=2)
             for r1 in range(2):
+                if wc == 0:
+                    nc.sync.dma_start(out=dp_rows(wc, r1), in_=pairs[:, r1, 2:6, :], max_dma_last_dim=4096)
+                    continue
                 for hf in range(2):
                     q = (2 * wc + hf + 1) % 4
                     for c1 in range(2):
-                        nc.sync.dma_start(out=dp_rows(wc, r1)[2 * hf + c1 : P : 4], in_=rows[:, r1, :, q, c1, :])
+                        nc.sync.dma_start(out=dp_rows(wc, r1)[2 * hf + c1 : P : 4], in_=rows[:, r1, q, c1, :])
 
-        def load_z(b, wr, sh):
-            slot = 8 * b + (2 * wr + sh + 1) % 8
-            nc.sync.dma_start(
-                out=z_raw[:, 512 * slot : 512 * slot + 512],
-                in_=z_heads[b, 2 * wr : 2 * wr + 2, :, 32 * sh : 32 * sh + 32, :].rearrange("w h (r s) d -> (w h) r (s d)", r=2),
-            )
+        def load_z(sh, r1, r0):
+            src = z_heads.rearrange("b (wr wc) h (sh r1 r0 s) d -> sh r1 r0 (wc h) (b wr) (s d)", wc=2, sh=2, r1=2, r0=2)
+            dst = z_raw[:, 512 * (sh + 1) : 512 * (sh + 16)].rearrange("p (j r n) -> p j r n", r=2, n=256)[:, 0:15:2, r1]
+            nc.sync.dma_start(out=dst[r0:P:2], in_=src[sh, r1, r0])
 
         copy_on = {"s": nc.scalar.copy, "v": nc.vector.tensor_copy}
 
@@ -127,7 +129,7 @@ def tile_functatransformer_pb_v_kernel(tc, z_heads, x, Wo, bo, grad_out, out_0, 
         def store0(quarter, s, sh, lo=0, hi=16):
             half, r = divmod(quarter, 2)
             view = out_0[:, :, 8 * quarter : 8 * quarter + 8].rearrange("b w h (sh s i) d -> sh s (b w) h (i d)", sh=2, i=8)
-            first = 64 * sh + s
+            first = 64 * sh + 2 * (s % 2) + s // 2
             src = st0[half][first + 4 * lo : first + 4 * hi - 3 : 4, 8 * r : 8 * r + 8]
             nc.sync.dma_start(out=view[sh, s, lo:hi], in_=src.rearrange("p h i d -> p h (i d)"))
 
@@ -138,18 +140,22 @@ def tile_functatransformer_pb_v_kernel(tc, z_heads, x, Wo, bo, grad_out, out_0, 
             )
 
         def z_sort(a, c0):
-            src = z_raw[:].bitcast(F32).rearrange("p (j c dhi a w) -> p c a dhi j w", c=2, dhi=4, a=2, w=2)
-            dst = z_srt[a][:].rearrange("p w m n -> p (w m n)").bitcast(F32).rearrange("p (w dhi c j) -> p c dhi j w", w=2, dhi=4, c=2)
-            nc.vector.tensor_copy(out=dst[:, c0], in_=src[:, c0, a])
+            words = z_raw[:].bitcast(F32)
+            dst = z_srt[a][:].rearrange("p w m n -> p (w m n)").bitcast(F32)
+            dst = dst.rearrange("p (w dhi c b j) -> p c dhi b j w", w=2, dhi=4, c=2, b=2)[:, c0]
+            src = words[:, 0 : 16 * 256].rearrange("p (b j c dhi a w) -> p c a dhi b j w", b=2, c=2, dhi=4, a=2, w=2)[:, c0, a]
+            nc.vector.tensor_copy(out=dst[:, :, :, 8:64], in_=src[:, :, :, 8:64])
+            last = words[:, 256 : 17 * 256].rearrange("p (b j c dhi a w) -> p c a dhi b j w", b=2, c=2, dhi=4, a=2, w=2)[:, c0, a]
+            nc.vector.tensor_copy(out=dst[:, :, :, 0:8], in_=last[:, :, :, 56:64])
 
         def z_tile(k, eng):
             a, w, e = k // 4, k // 2 % 2, k % 2
-            bank = psum.tile([P, 8, P], BF16, name="bank")
+            bank = psum.tile([P, 64, 8, 2], BF16, name="bank")
             for m in range(8):
-                nc.tensor.matmul(bank[:, m, :], z_srt[a][:, w, m, e : 256 : 2], ident_bf[:], start=True, stop=True)
+                nc.tensor.matmul(bank[:, :, m, :], z_srt[a][:, w, m, e : 256 : 2], ident_bf[:], start=True, stop=True)
             copy_on[eng](
-                out=z_g[k // 2][:, 1024 * e : 1024 * e + 1024].bitcast(F32).rearrange("p (x u m) -> p u x m", u=2, m=4),
-                in_=bank[:].rearrange("p m n -> p (m n)").bitcast(F32).rearrange("p (u m x) -> p u x m", u=2, m=4),
+                out=z_g[k // 2][:, 1024 * e : 1024 * e + 1024].bitcast(F32),
+                in_=bank[:].rearrange("p x m r -> p (x m r)").bitcast(F32),
             )
 
         def out1_pass(acc, k, n, wc):
@@ -169,10 +175,10 @@ def tile_functatransformer_pb_v_kernel(tc, z_heads, x, Wo, bo, grad_out, out_0, 
         load_dp(1)
         for c in range(4):
             load_wo(c)
-        for b in range(2):
-            for wr in range(4):
-                for sh in range(2):
-                    load_z(b, wr, sh)
+        for sh in range(2):
+            for r1 in range(2):
+                for r0 in range(2):
+                    load_z(sh, r1, r0)
 
         make_identity(nc, ident[:])
         pv = perm[:].rearrange("p (hc sh b wr r0) -> p hc b wr sh r0", hc=4, b=2, wr=4, sh=2)
@@ -250,7 +256,7 @@ def tile_functatransformer_pb_v_kernel(tc, z_heads, x, Wo, bo, grad_out, out_0, 
         dt_interleave(1, 0)
         for c in range(2, 4):
             for g in range(2):
-                wo_transposes(c, g, "svsv"[2 * c + g - 4])
+                wo_transposes(c, g, "sssv"[2 * c + g - 4])
         q_wo_quarter(0, 2)
         q_wo_quarter(1, 2)
         q_wo_quarter(0, 3)
@@ -258,34 +264,32 @@ def tile_functatransformer_pb_v_kernel(tc, z_heads, x, Wo, bo, grad_out, out_0, 
         out0_banks(0, range(3, 4), "s")
         out0_stores(0)
         out0_quarter(1, "ssss")
-        q_dt(0, 0)
-        q_dt(1, 0)
         z_sort(0, 0)
         z_sort(0, 1)
         out0_quarter(2, "ssss")
-        dt_interleave(1, 1)
-        z_sort(1, 0)
-        z_sort(1, 1)
-        out0_quarter(3, "ssss")
+        q_dt(0, 0)
+        q_dt(1, 0)
         z_tile(0, "v")
         z_tile(1, "s")
-        q_dt(0, 1)
+        dt_interleave(1, 1)
         q_z(0)
+        out0_quarter(3, "ssss")
+        q_dt(0, 1)
+        q_dt(1, 1)
         z_tile(2, "s")
         z_tile(3, "s")
-        q_dt(1, 1)
+        z_sort(1, 0)
+        z_sort(1, 1)
         q_z(1)
-        z_tile(4, "v")
-        z_tile(5, "s")
         for k in range(8):
             for n in range(2):
-                out1_half(k, n, "vssvsvsvvssvsvsv"[2 * k + n])
-                if k in (0, 4) and n == 0:
-                    q_z(k // 4 + 2)
+                out1_half(k, n, "ssvsvssvvssvsvsv"[2 * k + n])
+                if k in (2, 4) and n == 0:
+                    q_z(k // 2 + 1)
                 if k >= 7:
                     store1(k, 512 * n, 512 * n + 512)
             if k < 7:
                 store1(k, 0, E)
-            if k == 3:
-                z_tile(6, "v")
-                z_tile(7, "s")
+            if k in (1, 3):
+                z_tile(k + 3, "v")
+                z_tile(k + 4, "s")

@@ -264,31 +264,35 @@ def tile_functatransformer_pb_v_kernel(tc, z_heads, x, Wo, bo, grad_out, out_0, 
         out0_banks(0, range(3, 4), "s")
         out0_stores(0)
         out0_quarter(1, "ssss")
+        q_dt(0, 0)
+        q_dt(1, 0)
         z_sort(0, 0)
         z_sort(0, 1)
         out0_quarter(2, "ssss")
-        q_dt(0, 0)
-        q_dt(1, 0)
+        out0_banks(3, range(2), "ss")
+        dt_interleave(1, 1)
         z_tile(0, "v")
         z_tile(1, "s")
-        dt_interleave(1, 1)
-        q_z(0)
-        out0_quarter(3, "ssss")
         q_dt(0, 1)
+        q_z(0)
+        out0_banks(3, range(2, 4), "ss")
+        out0_stores(3)
         q_dt(1, 1)
+        z_sort(1, 0)
         z_tile(2, "s")
         z_tile(3, "s")
-        z_sort(1, 0)
         z_sort(1, 1)
         q_z(1)
         for k in range(8):
             for n in range(2):
-                out1_half(k, n, "ssvsvssvvssvsvsv"[2 * k + n])
+                out1_half(k, n, "sssvvssvvssvsvsv"[2 * k + n])
                 if k in (2, 4) and n == 0:
                     q_z(k // 2 + 1)
                 if k >= 7:
                     store1(k, 512 * n, 512 * n + 512)
-            if k < 7:
+            if k in (1,):
+                nc.sync.dma_start(out=out1_rows[:, k - 1 : k + 1, :], in_=st1[k // 2][:])
+            if 2 <= k < 7:
                 store1(k, 0, E)
             if k in (1, 3):
                 z_tile(k + 3, "v")

@@ -14,17 +14,19 @@ P = 128
 E = 1024
 FLOPS = 2 * 2 * E * E * E
 BYTES = 3 * 2 * E * E + 2 * 4 * E * E
+STEPPED_QUARTERS = 3
 
 
 def tile_functatransformer_pb_v_kernel(tc, z_heads, x, Wo, bo, grad_out, out_0, out_1):
     nc = tc.nc
+    scalar, vector = nc.scalar.copy, nc.vector.tensor_copy
     with ExitStack() as ctx:
         keep = ctx.enter_context(tc.tile_pool(name="keep", bufs=1))
         psum = ctx.enter_context(tc.psum_pool(name="psum", bufs=8))
         ctx.enter_context(tc.manual_schedule())
 
-        def tiles(name, shape, dtype, n0, n1):
-            return [[keep.tile(shape, dtype, name=f"{name}{a}{b}", align_bytes=64) for b in range(n1)] for a in range(n0)]
+        def tiles(name, shape, dtype):
+            return [[keep.tile(shape, dtype, name=f"{name}{a}{b}", align_bytes=64) for b in range(2)] for a in range(2)]
 
         wo_raw = [keep.tile([P, 2, E], BF16, name=f"wo_raw{c}", align_bytes=64) for c in range(4)]
         wo_srt = {}
@@ -35,265 +37,253 @@ def tile_functatransformer_pb_v_kernel(tc, z_heads, x, Wo, bo, grad_out, out_0, 
         ident = keep.tile([P, P], F32, name="ident", align_bytes=64)
         ident_bf = keep.tile([P, P], BF16, name="ident_bf", align_bytes=64)
         perm = keep.tile([P, P], F32, name="perm", align_bytes=64)
-        wo_g, wo_c, wo_s = tiles("wo_g", [P, 2048], BF16, 2, 2), tiles("wo_c", [P, 512], U32, 2, 2), tiles("wo_s", [P, 512], U8, 2, 2)
+        wo_g, wo_c, wo_s = tiles("wo_g", [P, 2048], BF16), tiles("wo_c", [P, 512], U32), tiles("wo_s", [P, 512], U8)
         df_g = [keep.tile([P, 2, 2048], BF16, name=f"df_g{g}", align_bytes=64) for g in range(2)]
-        df_c, df_s = tiles("df_c", [P, 512], U32, 2, 2), tiles("df_s", [P, 512], U8, 2, 2)
-        dt_g, dt_c, dt_s = tiles("dt_g", [P, 2048], BF16, 2, 2), tiles("dt_c", [P, 512], U32, 2, 2), tiles("dt_s", [P, 512], U8, 2, 2)
-        z_g = [keep.tile([P, 2048], BF16, name=f"z_g{k % 2}", align_bytes=64) for k in range(4)]
-        z_c = [keep.tile([P, 512], U32, name=f"z_c{k}", align_bytes=64) for k in range(4)]
-        z_s = [keep.tile([P, 512], U8, name=f"z_s{k}", align_bytes=64) for k in range(4)]
+        df_c, df_s = tiles("df_c", [P, 512], U32), tiles("df_s", [P, 512], U8)
+        dt_g, dt_c, dt_s = tiles("dt_g", [P, 2048], BF16), tiles("dt_c", [P, 512], U32), tiles("dt_s", [P, 512], U8)
+        z_g = [keep.tile([P, 2048], BF16, name=f"z_g{j % 2}", align_bytes=64) for j in range(4)]
+        z_c = [keep.tile([P, 512], U32, name=f"z_c{j}", align_bytes=64) for j in range(4)]
+        z_s = [keep.tile([P, 512], U8, name=f"z_s{j}", align_bytes=64) for j in range(4)]
         st0 = [keep.tile([P, 16, 8, 32], F32, name=f"st0_{n}", align_bytes=64) for n in range(2)]
-        st1 = [keep.tile([P, 2, E], F32, name=f"st1_{m}", align_bytes=64) for m in range(4)]
+        st1 = [keep.tile([P, 2, E], F32, name=f"st1_{j}", align_bytes=64) for j in range(4)]
 
-        def load_wo(c):
-            nc.sync.dma_start(out=wo_raw[c][:], in_=Wo[256 * c : 256 * c + 256, :].rearrange("(n p) e -> p n e", n=2))
-
-        def dp_rows(wc, r1):
-            return dp_raw[wc][:, 0, :] if r1 == 0 else dp_low[wc][:]
+        def dp_rows(wc, r0):
+            return dp_raw[wc][:, 0, :] if r0 == 0 else dp_low[wc][:]
 
         def load_dp(wc):
-            rows = grad_out.rearrange("b (ii r1 r0) (q c1 c0) e -> (b ii r1) r0 q c1 (c0 e)", r1=2, r0=2, c1=2, c0=2)
             pairs = grad_out.rearrange("b (i r0) (c c0) e -> (b i) r0 c (c0 e)", r0=2, c0=2)
-            for r1 in range(2):
+            for r0 in range(2):
                 if wc == 0:
-                    nc.sync.dma_start(out=dp_rows(wc, r1), in_=pairs[:, r1, 2:6, :], max_dma_last_dim=4096)
-                    continue
-                for hf in range(2):
-                    q = (2 * wc + hf + 1) % 4
-                    for c1 in range(2):
-                        nc.sync.dma_start(out=dp_rows(wc, r1)[2 * hf + c1 : P : 4], in_=rows[:, r1, q, c1, :])
+                    nc.sync.dma_start(out=dp_rows(wc, r0), in_=pairs[:, r0, 2:6, :], max_dma_last_dim=4096)
+                else:
+                    for c in range(4):
+                        nc.sync.dma_start(out=dp_rows(wc, r0)[c:P:4], in_=pairs[:, r0, (6 + c) % 8, :])
+
+        def load_wo(quarter):
+            rows = Wo[256 * quarter : 256 * quarter + 256, :].rearrange("(n p) e -> p n e", n=2)
+            nc.sync.dma_start(out=wo_raw[quarter][:], in_=rows)
 
         def load_z(sh, r1, r0):
             src = z_heads.rearrange("b (wr wc) h (sh r1 r0 s) d -> sh r1 r0 (wc h) (b wr) (s d)", wc=2, sh=2, r1=2, r0=2)
             dst = z_raw[:, 512 * (sh + 1) : 512 * (sh + 16)].rearrange("p (j r n) -> p j r n", r=2, n=256)[:, 0:15:2, r1]
             nc.sync.dma_start(out=dst[r0:P:2], in_=src[sh, r1, r0])
 
-        copy_on = {"s": nc.scalar.copy, "v": nc.vector.tensor_copy}
-
-        def wo_transposes(c, g, eng):
-            bank = psum.tile([P, 2, 2, P], F32, name="bank")
-            for n in range(2):
-                for u in range(2):
-                    if c < 2:
-                        words = wo_raw[c][:, n, :].bitcast(F32)[:, 256 * g + u : 256 * g + 256 : 2]
-                    else:
-                        words = wo_srt[c][:].rearrange("p (n g u j) -> p n g u j", n=2, g=2, u=2)[:, n, g, u, :]
-                    nc.tensor.transpose(bank[:, u, n, :], words, ident[:])
-            half, r = divmod(c, 2)
-            dst = wo_g[g][half][:].bitcast(F32).rearrange("p (r n q u) -> p r n q u", r=2, n=2, u=2)[:, r]
-            copy_on[eng](out=dst, in_=bank[:].rearrange("p u n q -> p n q u"))
-
-        def wo_sort(c):
-            wo_srt[c] = keep.tile([P, 2 * 2 * 2 * P], F32, name="spare", bufs=2, align_bytes=64)
-            nc.vector.tensor_copy(
-                out=wo_srt[c][:].rearrange("p (m u j) -> p m u j", u=2, j=P),
-                in_=wo_raw[c][:].rearrange("p n e -> p (n e)").bitcast(F32).rearrange("p (m j u) -> p m u j", u=2, j=P),
-            )
-
-        def dp_transposes(wc, r1, g, eng):
+        def dp_transposes(wc, r0, g):
             bank = psum.tile([P, 2, 2, P], F32, name="bank")
             for c0 in range(2):
-                words = dp_rows(wc, r1)[:, E * c0 : E * c0 + E].bitcast(F32)
+                words = dp_rows(wc, r0)[:, E * c0 : E * c0 + E].bitcast(F32)
                 for u in range(2):
                     nc.tensor.transpose(bank[:, u, c0, :], words[:, 256 * g + u : 256 * g + 256 : 2], perm[:])
             dst = df_g[g][:].rearrange("p c n -> p (c n)").bitcast(F32)
-            dst = dst.rearrange("p (x w r1 r0 u) -> p x w r1 r0 u", w=2, r1=2, r0=2, u=2)[:, :, wc, r1, :, :]
-            copy_on[eng](out=dst, in_=bank[:].rearrange("p u c (x r0) -> p (c x) r0 u", r0=2))
+            dst = dst.rearrange("p (x wc r0 r1 u) -> p x wc r0 r1 u", wc=2, r0=2, r1=2, u=2)[:, :, wc, r0, :, :]
+            scalar(out=dst, in_=bank[:].rearrange("p u c (x r1) -> p (c x) r1 u", r1=2))
+
+        def wo_sort(quarter):
+            wo_srt[quarter] = keep.tile([P, 2 * 2 * 2 * P], F32, name="spare", bufs=2, align_bytes=64)
+            words = wo_raw[quarter][:].rearrange("p n e -> p (n e)").bitcast(F32)
+            vector(
+                out=wo_srt[quarter][:].rearrange("p (m u j) -> p m u j", u=2, j=P),
+                in_=words.rearrange("p (m j u) -> p m u j", u=2, j=P),
+            )
+
+        def wo_transposes(quarter, g, copy):
+            bank = psum.tile([P, 2, 2, P], F32, name="bank")
+            for n in range(2):
+                for u in range(2):
+                    if quarter < STEPPED_QUARTERS:
+                        words = wo_raw[quarter][:, n, :].bitcast(F32)[:, 256 * g + u : 256 * g + 256 : 2]
+                    else:
+                        words = wo_srt[quarter][:].rearrange("p (n g u j) -> p n g u j", n=2, g=2, u=2)[:, n, g, u, :]
+                    nc.tensor.transpose(bank[:, u, n, :], words, ident[:])
+            half, r = divmod(quarter, 2)
+            dst = wo_g[g][half][:].bitcast(F32).rearrange("p (r n q u) -> p r n q u", r=2, n=2, u=2)[:, r]
+            copy(out=dst, in_=bank[:].rearrange("p u n q -> p n q u"))
+
+        def quantise_df(c0):
+            for g in range(2):
+                nc.vector.quantize_mx(out=df_c[g][c0][:].bitcast(E5M2), scales=df_s[g][c0][:], in_=df_g[g][:, c0, :])
+
+        def quantise_wo(quarter):
+            half, r = divmod(quarter, 2)
+            for g in range(2):
+                nc.vector.quantize_mx(
+                    out=wo_c[g][half][:, 256 * r : 256 * r + 256].bitcast(E4M3),
+                    scales=wo_s[g][half][:, 256 * r : 256 * r + 256],
+                    in_=wo_g[g][half][:, 1024 * r : 1024 * r + 1024],
+                )
+
+        def out0_banks(quarter, banks):
+            half, r = divmod(quarter, 2)
+            for bank in banks:
+                c0, hf = divmod(bank, 2)
+                acc = psum.tile([P, 2, 256], F32, name="bank")
+                for c1 in range(2):
+                    cols = slice(128 * (2 * hf + c1), 128 * (2 * hf + c1) + 128)
+                    for g in range(2):
+                        nc.tensor.matmul_mx(
+                            out=acc[:, c1, :],
+                            lhsT=df_c[g][c0][:, cols].bitcast(E5M2),
+                            lhsT_scale=df_s[g][c0][:, cols],
+                            rhs=wo_c[g][half][:, 256 * r : 256 * r + 256].bitcast(E4M3),
+                            rhs_scale=wo_s[g][half][:, 256 * r : 256 * r + 256],
+                            start=(g == 0),
+                            stop=(g == 1),
+                        )
+                dst = st0[half][:, 8 * r : 8 * r + 8].rearrange("p h (t c) d -> p h t c d", c=2)[:, :, 2 * hf : 2 * hf + 2, c0, :]
+                scalar(out=dst, in_=acc[:].rearrange("p i (h d) -> p h i d", d=32))
+
+        def store0(quarter, row, sh, lo, hi):
+            half, r = divmod(quarter, 2)
+            view = out_0[:, :, 8 * quarter : 8 * quarter + 8].rearrange("b w h (sh s i) d -> sh s (b w) h (i d)", sh=2, i=8)
+            first = 64 * sh + 2 * (row % 2) + row // 2
+            src = st0[half][first + 4 * lo : first + 4 * hi - 3 : 4, 8 * r : 8 * r + 8]
+            nc.sync.dma_start(out=view[sh, row, lo:hi], in_=src.rearrange("p h i d -> p h (i d)"))
+
+        def out0_stores(quarter):
+            for row in range(4):
+                for sh in range(2):
+                    store0(quarter, row, sh, 0, 8 if (quarter, row, sh) == (0, 0, 0) else 16)
+            if quarter == 3:
+                store0(0, 0, 0, 8, 16)
 
         def dp_join(wc):
             dst = dp_raw[wc][:, 1, :].rearrange("p (c n e) -> p n c e", c=2, n=2)
             src = dp_low[wc][:].rearrange("p (c n e) -> p n c e", c=2, n=2)
             for n in range(2):
-                nc.vector.tensor_copy(out=dst[:, n], in_=src[:, n])
-
-        def quant(codes, scales, src, fmt):
-            nc.vector.quantize_mx(out=codes[:].bitcast(fmt), scales=scales[:], in_=src)
-
-        def out0_pair(t, c0, quarter, eng):
-            half, r = divmod(quarter, 2)
-            acc = psum.tile([P, 2, 256], F32, name="bank")
-            for i in range(2):
-                for g in range(2):
-                    nc.tensor.matmul_mx(
-                        out=acc[:, i, :],
-                        lhsT=df_c[g][c0][:, 128 * (t + i) : 128 * (t + i) + 128].bitcast(E5M2),
-                        lhsT_scale=df_s[g][c0][:, 128 * (t + i) : 128 * (t + i) + 128],
-                        rhs=wo_c[g][half][:, 256 * r : 256 * r + 256].bitcast(E4M3),
-                        rhs_scale=wo_s[g][half][:, 256 * r : 256 * r + 256],
-                        start=(g == 0),
-                        stop=(g == 1),
-                    )
-            dst = st0[half][:, 8 * r : 8 * r + 8].rearrange("p h (t c) d -> p h t c d", c=2)[:, :, t : t + 2, c0, :]
-            copy_on[eng](out=dst, in_=acc[:].rearrange("p i (h d) -> p h i d", d=32))
-
-        def store0(quarter, s, sh, lo=0, hi=16):
-            half, r = divmod(quarter, 2)
-            view = out_0[:, :, 8 * quarter : 8 * quarter + 8].rearrange("b w h (sh s i) d -> sh s (b w) h (i d)", sh=2, i=8)
-            first = 64 * sh + 2 * (s % 2) + s // 2
-            src = st0[half][first + 4 * lo : first + 4 * hi - 3 : 4, 8 * r : 8 * r + 8]
-            nc.sync.dma_start(out=view[sh, s, lo:hi], in_=src.rearrange("p h i d -> p h (i d)"))
+                vector(out=dst[:, n], in_=src[:, n])
 
         def dt_interleave(wc, n):
-            nc.vector.tensor_copy(
+            vector(
                 out=dt_g[wc][n][:].rearrange("p (e c r) -> p e c r", c=2, r=2),
                 in_=dp_raw[wc][:].rearrange("p r (c e) -> p e c r", c=2)[:, 512 * n : 512 * n + 512],
             )
 
+        def quantise_dt(wc, n):
+            nc.vector.quantize_mx(out=dt_c[wc][n][:].bitcast(E5M2), scales=dt_s[wc][n][:], in_=dt_g[wc][n][:])
+
         def z_sort(a, c0):
-            words = z_raw[:].bitcast(F32)
+            def slots(first):
+                words = z_raw[:].bitcast(F32)[:, 256 * first : 256 * (first + 16)]
+                return words.rearrange("p (b j c dhi a w) -> p c a dhi b j w", b=2, c=2, dhi=4, a=2, w=2)[:, c0, a]
+
             dst = z_srt[a][:].rearrange("p w m n -> p (w m n)").bitcast(F32)
             dst = dst.rearrange("p (w dhi c b j) -> p c dhi b j w", w=2, dhi=4, c=2, b=2)[:, c0]
-            src = words[:, 0 : 16 * 256].rearrange("p (b j c dhi a w) -> p c a dhi b j w", b=2, c=2, dhi=4, a=2, w=2)[:, c0, a]
-            nc.vector.tensor_copy(out=dst[:, :, :, 8:64], in_=src[:, :, :, 8:64])
-            last = words[:, 256 : 17 * 256].rearrange("p (b j c dhi a w) -> p c a dhi b j w", b=2, c=2, dhi=4, a=2, w=2)[:, c0, a]
-            nc.vector.tensor_copy(out=dst[:, :, :, 0:8], in_=last[:, :, :, 56:64])
+            vector(out=dst[:, :, :, 8:64], in_=slots(0)[:, :, :, 8:64])
+            vector(out=dst[:, :, :, 0:8], in_=slots(1)[:, :, :, 56:64])
 
-        def z_tile(k, eng):
+        def z_tile(k, copy):
             a, w, e = k // 4, k // 2 % 2, k % 2
             bank = psum.tile([P, 64, 8, 2], BF16, name="bank")
             for m in range(8):
                 nc.tensor.matmul(bank[:, :, m, :], z_srt[a][:, w, m, e : 256 : 2], ident_bf[:], start=True, stop=True)
-            copy_on[eng](
+            copy(
                 out=z_g[k // 2][:, 1024 * e : 1024 * e + 1024].bitcast(F32),
                 in_=bank[:].rearrange("p x m r -> p (x m r)").bitcast(F32),
             )
 
-        def out1_pass(acc, k, n, wc):
-            nc.tensor.matmul_mx(
-                out=acc[:],
-                lhsT=z_c[k // 2][:, 256 * (k % 2) + 128 * wc : 256 * (k % 2) + 128 * wc + 128].bitcast(E4M3),
-                lhsT_scale=z_s[k // 2][:, 256 * (k % 2) + 128 * wc : 256 * (k % 2) + 128 * wc + 128],
-                rhs=dt_c[wc][n][:].bitcast(E5M2),
-                rhs_scale=dt_s[wc][n][:],
-                start=(wc == 0),
-                stop=(wc == 1),
-            )
+        def quantise_z(j):
+            nc.vector.quantize_mx(out=z_c[j][:].bitcast(E4M3), scales=z_s[j][:], in_=z_g[j][:])
+
+        def out1_half(k, n, copy):
+            acc = psum.tile([P, 512], F32, name="bank")
+            for wc in range(2):
+                cols = slice(256 * (k % 2) + 128 * wc, 256 * (k % 2) + 128 * wc + 128)
+                nc.tensor.matmul_mx(
+                    out=acc[:],
+                    lhsT=z_c[k // 2][:, cols].bitcast(E4M3),
+                    lhsT_scale=z_s[k // 2][:, cols],
+                    rhs=dt_c[wc][n][:].bitcast(E5M2),
+                    rhs_scale=dt_s[wc][n][:],
+                    start=(wc == 0),
+                    stop=(wc == 1),
+                )
+            copy(out=st1[k // 2][:, k % 2, 512 * n : 512 * n + 512], in_=acc[:])
 
         out1_rows = out_1.rearrange("(m k) e -> m k e", k=8)
 
-        load_dp(0)
-        load_dp(1)
-        for c in range(4):
-            load_wo(c)
+        def store1(k, lo, hi):
+            nc.sync.dma_start(out=out1_rows[:, k, lo:hi], in_=st1[k // 2][:, k % 2, lo:hi])
+
+        for wc in range(2):
+            load_dp(wc)
+        for quarter in range(4):
+            load_wo(quarter)
         for sh in range(2):
             for r1 in range(2):
                 for r0 in range(2):
                     load_z(sh, r1, r0)
 
         make_identity(nc, ident[:])
-        pv = perm[:].rearrange("p (hc sh b wr r0) -> p hc b wr sh r0", hc=4, b=2, wr=4, sh=2)
-        iv = ident[:].rearrange("p (b k m r0 hc) -> p hc b k m r0", b=2, k=4, m=2, r0=2)
+        pv = perm[:].rearrange("p (hc sh b wr r1) -> p hc b wr sh r1", hc=4, b=2, wr=4, sh=2)
+        iv = ident[:].rearrange("p (b k m r1 hc) -> p hc b k m r1", b=2, k=4, m=2, r1=2)
         for b in range(2):
-            nc.vector.tensor_copy(out=pv[:, :, b, :, 0, :], in_=iv[:, :, b, :, 1, :])
-            nc.vector.tensor_copy(out=pv[:, :, b, 0:3, 1, :], in_=iv[:, :, b, 1:4, 0, :])
-            nc.vector.tensor_copy(out=pv[:, :, b, 3, 1, :], in_=iv[:, :, b, 0, 0, :])
-        nc.vector.tensor_copy(out=ident_bf[:], in_=ident[:])
-
-        def q_wo_quarter(g, quarter):
-            half, r = divmod(quarter, 2)
-            nc.vector.quantize_mx(
-                out=wo_c[g][half][:, 256 * r : 256 * r + 256].bitcast(E4M3),
-                scales=wo_s[g][half][:, 256 * r : 256 * r + 256],
-                in_=wo_g[g][half][:, 1024 * r : 1024 * r + 1024],
-            )
-
-        def out0_banks(quarter, banks, engs):
-            for i, eng in zip(banks, engs):
-                out0_pair(2 * (i % 2), i // 2, quarter, eng)
-
-        def out0_stores(quarter):
-            for s in range(4):
-                for sh in (1, 0):
-                    store0(quarter, s, sh, hi=8 if (quarter, s, sh) == (0, 0, 0) else 16)
-            if quarter == 3:
-                store0(0, 0, 0, lo=8)
-
-        def out0_quarter(quarter, engs):
-            out0_banks(quarter, range(4), engs)
-            out0_stores(quarter)
-
-        def out1_half(k, n, eng):
-            acc = psum.tile([P, 512], F32, name="bank")
-            for wc in range(2):
-                out1_pass(acc, k, n, wc)
-            copy_on[eng](out=st1[k // 2][:, k % 2, 512 * n : 512 * n + 512], in_=acc[:])
-
-        def store1(k, lo, hi):
-            nc.sync.dma_start(out=out1_rows[:, k, lo:hi], in_=st1[k // 2][:, k % 2, lo:hi])
-
-        def q_df(g, c0):
-            quant(df_c[g][c0], df_s[g][c0], df_g[g][:, c0, :], E5M2)
-
-        def q_dt(wc, n):
-            quant(dt_c[wc][n], dt_s[wc][n], dt_g[wc][n][:], E5M2)
-
-        def q_z(k):
-            quant(z_c[k], z_s[k], z_g[k][:], E4M3)
+            vector(out=pv[:, :, b, :, 0, :], in_=iv[:, :, b, :, 1, :])
+            vector(out=pv[:, :, b, 0:3, 1, :], in_=iv[:, :, b, 1:4, 0, :])
+            vector(out=pv[:, :, b, 3, 1, :], in_=iv[:, :, b, 0, 0, :])
+        vector(out=ident_bf[:], in_=ident[:])
 
         for wc in range(2):
-            for r1 in range(2):
+            for r0 in range(2):
                 for g in range(2):
-                    dp_transposes(wc, r1, g, "ssssssss"[4 * wc + 2 * r1 + g])
+                    dp_transposes(wc, r0, g)
             dp_join(wc)
             if wc == 0:
                 dt_interleave(0, 0)
                 dt_interleave(0, 1)
-        for c in range(2):
+        for quarter in range(STEPPED_QUARTERS):
             for g in range(2):
-                wo_transposes(c, g, "s")
-            if c == 0:
-                q_df(0, 0)
-                q_df(1, 0)
-                q_wo_quarter(0, 0)
-                q_wo_quarter(1, 0)
-                q_df(0, 1)
-                q_df(1, 1)
-        wo_sort(2)
+                wo_transposes(quarter, g, scalar)
+            if quarter == 0:
+                quantise_df(0)
+                quantise_wo(0)
+                quantise_df(1)
+
+        quantise_wo(1)
         wo_sort(3)
-        q_wo_quarter(0, 1)
-        q_wo_quarter(1, 1)
-        out0_banks(0, range(3), "sss")
-        dt_interleave(1, 0)
-        for c in range(2, 4):
-            for g in range(2):
-                wo_transposes(c, g, "sssv"[2 * c + g - 4])
-        q_wo_quarter(0, 2)
-        q_wo_quarter(1, 2)
-        q_wo_quarter(0, 3)
-        q_wo_quarter(1, 3)
-        out0_banks(0, range(3, 4), "s")
+        quantise_wo(2)
+        out0_banks(0, range(4))
         out0_stores(0)
-        out0_quarter(1, "ssss")
-        q_dt(0, 0)
-        q_dt(1, 0)
+        dt_interleave(1, 0)
+        quantise_dt(0, 0)
+        out0_banks(1, range(4))
+        out0_stores(1)
+        quantise_dt(1, 0)
+        for g in range(2):
+            wo_transposes(3, g, vector)
+        quantise_wo(3)
         z_sort(0, 0)
         z_sort(0, 1)
-        out0_quarter(2, "ssss")
-        out0_banks(3, range(2), "ss")
+        out0_banks(2, range(4))
+        out0_stores(2)
         dt_interleave(1, 1)
-        z_tile(0, "v")
-        z_tile(1, "s")
-        q_dt(0, 1)
-        q_z(0)
-        out0_banks(3, range(2, 4), "ss")
+        out0_banks(3, range(2))
+        z_tile(0, vector)
+        z_tile(1, scalar)
+        quantise_dt(0, 1)
+        quantise_z(0)
+        out0_banks(3, range(2, 4))
         out0_stores(3)
-        q_dt(1, 1)
+        quantise_dt(1, 1)
         z_sort(1, 0)
-        z_tile(2, "s")
-        z_tile(3, "s")
+        z_tile(2, scalar)
+        z_tile(3, scalar)
         z_sort(1, 1)
-        q_z(1)
+        quantise_z(1)
+
         for k in range(8):
-            for n in range(2):
-                out1_half(k, n, "sssvvssvvssvsvsv"[2 * k + n])
-                if k in (2, 4) and n == 0:
-                    q_z(k // 2 + 1)
-                if k >= 7:
-                    store1(k, 512 * n, 512 * n + 512)
-            if k in (1,):
-                nc.sync.dma_start(out=out1_rows[:, k - 1 : k + 1, :], in_=st1[k // 2][:])
-            if 2 <= k < 7:
+            behind_z_run = k in (2, 4)
+            out1_half(k, 0, vector if behind_z_run else scalar)
+            if behind_z_run:
+                quantise_z(k // 2 + 1)
+            if k >= 4:
+                store1(k, 0, 512)
+            out1_half(k, 1, scalar if behind_z_run or k == 0 else vector)
+            if k == 1:
+                nc.sync.dma_start(out=out1_rows[:, 0:2, :], in_=st1[0][:])
+            elif k >= 4:
+                store1(k, 512, E)
+            elif k > 1:
                 store1(k, 0, E)
             if k in (1, 3):
-                z_tile(k + 3, "v")
-                z_tile(k + 4, "s")
+                z_tile(k + 3, vector)
+                z_tile(k + 4, scalar)

from contextlib import ExitStack

import concourse.mybir as mybir
from concourse.masks import make_identity

F32 = mybir.dt.float32
BF16 = mybir.dt.bfloat16
U32 = mybir.dt.uint32
U8 = mybir.dt.uint8
E4M3 = mybir.dt.float8_e4m3fn_x4
E5M2 = mybir.dt.float8_e5m2_x4

P = 128
E = 1024
FLOPS = 2 * 2 * E * E * E
BYTES = 3 * 2 * E * E + 2 * 4 * E * E
STEPPED_QUARTERS = 3


def tile_functatransformer_pb_v_kernel(tc, z_heads, x, Wo, bo, grad_out, out_0, out_1):
    nc = tc.nc
    scalar, vector = nc.scalar.copy, nc.vector.tensor_copy
    with ExitStack() as ctx:
        keep = ctx.enter_context(tc.tile_pool(name="keep", bufs=1))
        psum = ctx.enter_context(tc.psum_pool(name="psum", bufs=8))
        ctx.enter_context(tc.manual_schedule())

        def tiles(name, shape, dtype):
            return [[keep.tile(shape, dtype, name=f"{name}{a}{b}", align_bytes=64) for b in range(2)] for a in range(2)]

        wo_raw = [keep.tile([P, 2, E], BF16, name=f"wo_raw{c}", align_bytes=64) for c in range(4)]
        wo_srt = {}
        dp_raw = [keep.tile([P, 2, 2 * E], BF16, name=f"dp_raw{w}", align_bytes=64) for w in range(2)]
        dp_low = [keep.tile([P, 2 * E], BF16, name="spare", bufs=2, align_bytes=64) for w in range(2)]
        z_raw = keep.tile([P, 17 * 512], BF16, name="z_raw", align_bytes=64)
        z_srt = [keep.tile([P, 2, 8, 256], BF16, name=f"z_srt{a}", align_bytes=64) for a in range(2)]
        ident = keep.tile([P, P], F32, name="ident", align_bytes=64)
        ident_bf = keep.tile([P, P], BF16, name="ident_bf", align_bytes=64)
        perm = keep.tile([P, P], F32, name="perm", align_bytes=64)
        wo_g, wo_c, wo_s = tiles("wo_g", [P, 2048], BF16), tiles("wo_c", [P, 512], U32), tiles("wo_s", [P, 512], U8)
        df_g = [keep.tile([P, 2, 2048], BF16, name=f"df_g{g}", align_bytes=64) for g in range(2)]
        df_c, df_s = tiles("df_c", [P, 512], U32), tiles("df_s", [P, 512], U8)
        dt_g, dt_c, dt_s = tiles("dt_g", [P, 2048], BF16), tiles("dt_c", [P, 512], U32), tiles("dt_s", [P, 512], U8)
        z_g = [keep.tile([P, 2048], BF16, name=f"z_g{j % 2}", align_bytes=64) for j in range(4)]
        z_c = [keep.tile([P, 512], U32, name=f"z_c{j}", align_bytes=64) for j in range(4)]
        z_s = [keep.tile([P, 512], U8, name=f"z_s{j}", align_bytes=64) for j in range(4)]
        st0 = [keep.tile([P, 16, 8, 32], F32, name=f"st0_{n}", align_bytes=64) for n in range(2)]
        st1 = [keep.tile([P, 2, E], F32, name=f"st1_{j}", align_bytes=64) for j in range(4)]

        def dp_rows(wc, r0):
            return dp_raw[wc][:, 0, :] if r0 == 0 else dp_low[wc][:]

        def load_dp(wc):
            pairs = grad_out.rearrange("b (i r0) (c c0) e -> (b i) r0 c (c0 e)", r0=2, c0=2)
            for r0 in range(2):
                if wc == 0:
                    nc.sync.dma_start(out=dp_rows(wc, r0), in_=pairs[:, r0, 2:6, :], max_dma_last_dim=4096)
                else:
                    for c in range(4):
                        nc.sync.dma_start(out=dp_rows(wc, r0)[c:P:4], in_=pairs[:, r0, (6 + c) % 8, :])

        def load_wo(quarter):
            rows = Wo[256 * quarter : 256 * quarter + 256, :].rearrange("(n p) e -> p n e", n=2)
            nc.sync.dma_start(out=wo_raw[quarter][:], in_=rows)

        def load_z(sh, r1, r0):
            src = z_heads.rearrange("b (wr wc) h (sh r1 r0 s) d -> sh r1 r0 (wc h) (b wr) (s d)", wc=2, sh=2, r1=2, r0=2)
            dst = z_raw[:, 512 * (sh + 1) : 512 * (sh + 16)].rearrange("p (j r n) -> p j r n", r=2, n=256)[:, 0:15:2, r1]
            nc.sync.dma_start(out=dst[r0:P:2], in_=src[sh, r1, r0])

        def dp_transposes(wc, r0, g):
            bank = psum.tile([P, 2, 2, P], F32, name="bank")
            for c0 in range(2):
                words = dp_rows(wc, r0)[:, E * c0 : E * c0 + E].bitcast(F32)
                for u in range(2):
                    nc.tensor.transpose(bank[:, u, c0, :], words[:, 256 * g + u : 256 * g + 256 : 2], perm[:])
            dst = df_g[g][:].rearrange("p c n -> p (c n)").bitcast(F32)
            dst = dst.rearrange("p (x wc r0 r1 u) -> p x wc r0 r1 u", wc=2, r0=2, r1=2, u=2)[:, :, wc, r0, :, :]
            scalar(out=dst, in_=bank[:].rearrange("p u c (x r1) -> p (c x) r1 u", r1=2))

        def wo_sort(quarter):
            wo_srt[quarter] = keep.tile([P, 2 * 2 * 2 * P], F32, name="spare", bufs=2, align_bytes=64)
            words = wo_raw[quarter][:].rearrange("p n e -> p (n e)").bitcast(F32)
            vector(
                out=wo_srt[quarter][:].rearrange("p (m u j) -> p m u j", u=2, j=P),
                in_=words.rearrange("p (m j u) -> p m u j", u=2, j=P),
            )

        def wo_transposes(quarter, g, copy):
            bank = psum.tile([P, 2, 2, P], F32, name="bank")
            for n in range(2):
                for u in range(2):
                    if quarter < STEPPED_QUARTERS:
                        words = wo_raw[quarter][:, n, :].bitcast(F32)[:, 256 * g + u : 256 * g + 256 : 2]
                    else:
                        words = wo_srt[quarter][:].rearrange("p (n g u j) -> p n g u j", n=2, g=2, u=2)[:, n, g, u, :]
                    nc.tensor.transpose(bank[:, u, n, :], words, ident[:])
            half, r = divmod(quarter, 2)
            dst = wo_g[g][half][:].bitcast(F32).rearrange("p (r n q u) -> p r n q u", r=2, n=2, u=2)[:, r]
            copy(out=dst, in_=bank[:].rearrange("p u n q -> p n q u"))

        def quantise_df(c0):
            for g in range(2):
                nc.vector.quantize_mx(out=df_c[g][c0][:].bitcast(E5M2), scales=df_s[g][c0][:], in_=df_g[g][:, c0, :])

        def quantise_wo(quarter):
            half, r = divmod(quarter, 2)
            for g in range(2):
                nc.vector.quantize_mx(
                    out=wo_c[g][half][:, 256 * r : 256 * r + 256].bitcast(E4M3),
                    scales=wo_s[g][half][:, 256 * r : 256 * r + 256],
                    in_=wo_g[g][half][:, 1024 * r : 1024 * r + 1024],
                )

        def out0_banks(quarter, banks):
            half, r = divmod(quarter, 2)
            for bank in banks:
                c0, hf = divmod(bank, 2)
                acc = psum.tile([P, 2, 256], F32, name="bank")
                for c1 in range(2):
                    cols = slice(128 * (2 * hf + c1), 128 * (2 * hf + c1) + 128)
                    for g in range(2):
                        nc.tensor.matmul_mx(
                            out=acc[:, c1, :],
                            lhsT=df_c[g][c0][:, cols].bitcast(E5M2),
                            lhsT_scale=df_s[g][c0][:, cols],
                            rhs=wo_c[g][half][:, 256 * r : 256 * r + 256].bitcast(E4M3),
                            rhs_scale=wo_s[g][half][:, 256 * r : 256 * r + 256],
                            start=(g == 0),
                            stop=(g == 1),
                        )
                dst = st0[half][:, 8 * r : 8 * r + 8].rearrange("p h (t c) d -> p h t c d", c=2)[:, :, 2 * hf : 2 * hf + 2, c0, :]
                scalar(out=dst, in_=acc[:].rearrange("p i (h d) -> p h i d", d=32))

        def store0(quarter, row, sh, lo, hi):
            half, r = divmod(quarter, 2)
            view = out_0[:, :, 8 * quarter : 8 * quarter + 8].rearrange("b w h (sh s i) d -> sh s (b w) h (i d)", sh=2, i=8)
            first = 64 * sh + 2 * (row % 2) + row // 2
            src = st0[half][first + 4 * lo : first + 4 * hi - 3 : 4, 8 * r : 8 * r + 8]
            nc.sync.dma_start(out=view[sh, row, lo:hi], in_=src.rearrange("p h i d -> p h (i d)"))

        def out0_stores(quarter):
            for row in range(4):
                for sh in range(2):
                    store0(quarter, row, sh, 0, 8 if (quarter, row, sh) == (0, 0, 0) else 16)
            if quarter == 3:
                store0(0, 0, 0, 8, 16)

        def dp_join(wc):
            dst = dp_raw[wc][:, 1, :].rearrange("p (c n e) -> p n c e", c=2, n=2)
            src = dp_low[wc][:].rearrange("p (c n e) -> p n c e", c=2, n=2)
            for n in range(2):
                vector(out=dst[:, n], in_=src[:, n])

        def dt_interleave(wc, n):
            vector(
                out=dt_g[wc][n][:].rearrange("p (e c r) -> p e c r", c=2, r=2),
                in_=dp_raw[wc][:].rearrange("p r (c e) -> p e c r", c=2)[:, 512 * n : 512 * n + 512],
            )

        def quantise_dt(wc, n):
            nc.vector.quantize_mx(out=dt_c[wc][n][:].bitcast(E5M2), scales=dt_s[wc][n][:], in_=dt_g[wc][n][:])

        def z_sort(a, c0):
            def slots(first):
                words = z_raw[:].bitcast(F32)[:, 256 * first : 256 * (first + 16)]
                return words.rearrange("p (b j c dhi a w) -> p c a dhi b j w", b=2, c=2, dhi=4, a=2, w=2)[:, c0, a]

            dst = z_srt[a][:].rearrange("p w m n -> p (w m n)").bitcast(F32)
            dst = dst.rearrange("p (w dhi c b j) -> p c dhi b j w", w=2, dhi=4, c=2, b=2)[:, c0]
            vector(out=dst[:, :, :, 8:64], in_=slots(0)[:, :, :, 8:64])
            vector(out=dst[:, :, :, 0:8], in_=slots(1)[:, :, :, 56:64])

        def z_tile(k, copy):
            a, w, e = k // 4, k // 2 % 2, k % 2
            bank = psum.tile([P, 64, 8, 2], BF16, name="bank")
            for m in range(8):
                nc.tensor.matmul(bank[:, :, m, :], z_srt[a][:, w, m, e : 256 : 2], ident_bf[:], start=True, stop=True)
            copy(
                out=z_g[k // 2][:, 1024 * e : 1024 * e + 1024].bitcast(F32),
                in_=bank[:].rearrange("p x m r -> p (x m r)").bitcast(F32),
            )

        def quantise_z(j):
            nc.vector.quantize_mx(out=z_c[j][:].bitcast(E4M3), scales=z_s[j][:], in_=z_g[j][:])

        def out1_half(k, n, copy):
            acc = psum.tile([P, 512], F32, name="bank")
            for wc in range(2):
                cols = slice(256 * (k % 2) + 128 * wc, 256 * (k % 2) + 128 * wc + 128)
                nc.tensor.matmul_mx(
                    out=acc[:],
                    lhsT=z_c[k // 2][:, cols].bitcast(E4M3),
                    lhsT_scale=z_s[k // 2][:, cols],
                    rhs=dt_c[wc][n][:].bitcast(E5M2),
                    rhs_scale=dt_s[wc][n][:],
                    start=(wc == 0),
                    stop=(wc == 1),
                )
            copy(out=st1[k // 2][:, k % 2, 512 * n : 512 * n + 512], in_=acc[:])

        out1_rows = out_1.rearrange("(m k) e -> m k e", k=8)

        def store1(k, lo, hi):
            nc.sync.dma_start(out=out1_rows[:, k, lo:hi], in_=st1[k // 2][:, k % 2, lo:hi])

        for wc in range(2):
            load_dp(wc)
        for quarter in range(4):
            load_wo(quarter)
        for sh in range(2):
            for r1 in range(2):
                for r0 in range(2):
                    load_z(sh, r1, r0)

        make_identity(nc, ident[:])
        pv = perm[:].rearrange("p (hc sh b wr r1) -> p hc b wr sh r1", hc=4, b=2, wr=4, sh=2)
        iv = ident[:].rearrange("p (b k m r1 hc) -> p hc b k m r1", b=2, k=4, m=2, r1=2)
        for b in range(2):
            vector(out=pv[:, :, b, :, 0, :], in_=iv[:, :, b, :, 1, :])
            vector(out=pv[:, :, b, 0:3, 1, :], in_=iv[:, :, b, 1:4, 0, :])
            vector(out=pv[:, :, b, 3, 1, :], in_=iv[:, :, b, 0, 0, :])
        vector(out=ident_bf[:], in_=ident[:])

        for wc in range(2):
            for r0 in range(2):
                for g in range(2):
                    dp_transposes(wc, r0, g)
            dp_join(wc)
            if wc == 0:
                dt_interleave(0, 0)
                dt_interleave(0, 1)
        for quarter in range(STEPPED_QUARTERS):
            for g in range(2):
                wo_transposes(quarter, g, scalar)
            if quarter == 0:
                quantise_df(0)
                quantise_wo(0)
                quantise_df(1)

        quantise_wo(1)
        wo_sort(3)
        quantise_wo(2)
        out0_banks(0, range(4))
        out0_stores(0)
        dt_interleave(1, 0)
        quantise_dt(0, 0)
        out0_banks(1, range(4))
        out0_stores(1)
        quantise_dt(1, 0)
        for g in range(2):
            wo_transposes(3, g, vector)
        quantise_wo(3)
        z_sort(0, 0)
        z_sort(0, 1)
        out0_banks(2, range(4))
        out0_stores(2)
        dt_interleave(1, 1)
        out0_banks(3, range(2))
        z_tile(0, vector)
        z_tile(1, scalar)
        quantise_dt(0, 1)
        quantise_z(0)
        out0_banks(3, range(2, 4))
        out0_stores(3)
        quantise_dt(1, 1)
        z_sort(1, 0)
        z_tile(2, scalar)
        z_tile(3, scalar)
        z_sort(1, 1)
        quantise_z(1)

        for k in range(8):
            behind_z_run = k in (2, 4)
            out1_half(k, 0, vector if behind_z_run else scalar)
            if behind_z_run:
                quantise_z(k // 2 + 1)
            if k >= 4:
                store1(k, 0, 512)
            out1_half(k, 1, scalar if behind_z_run or k == 0 else vector)
            if k == 1:
                nc.sync.dma_start(out=out1_rows[:, 0:2, :], in_=st1[0][:])
            elif k >= 4:
                store1(k, 512, E)
            elif k > 1:
                store1(k, 0, E)
            if k in (1, 3):
                z_tile(k + 3, vector)
                z_tile(k + 4, scalar)
